import numpy as np
import ml_dtypes


def mxq(x, axis, fmt="e4m3"):
    dtype, down = {"e4m3": (ml_dtypes.float8_e4m3fn, 7), "e5m2": (ml_dtypes.float8_e5m2, 14)}[fmt]
    v = np.moveaxis(np.asarray(x, np.float32).astype(ml_dtypes.bfloat16).astype(np.float64), axis, -1)
    blocks = v.reshape(v.shape[:-1] + (-1, 32))
    amax = np.abs(blocks).max(-1, keepdims=True)
    byte = np.maximum(np.where(amax > 0, np.frexp(amax)[1] - 1 + 127, 0) - down, 1)
    scale = np.exp2(byte - 127.0)
    codes = (blocks / scale).astype(np.float32).astype(dtype).astype(np.float64)
    return np.moveaxis((codes * scale).reshape(v.shape), -1, axis)


WIDE = False


def mx_kscale(k):
    if not WIDE:
        return np.ones(k)
    levels = np.array([10, -10, 5, -5, 0])
    if k % 512:
        return np.exp2(np.random.permutation(np.resize(levels, k // 32))).repeat(32)
    a = np.empty((k // 512, 16))
    for p in range(k // 512):
        a[p, :8] = np.random.permutation(np.resize(levels, 8))
        for g in range(8):
            far = levels[np.abs(levels - a[p, g]) >= 10]
            a[p, g + 8] = far[np.random.randint(len(far))]
    return np.exp2(a.ravel()).repeat(32)


BF16 = ml_dtypes.bfloat16


def bf(x):
    return np.asarray(x, np.float32).astype(BF16)


def f64(x):
    return np.asarray(x).astype(np.float64)


B, F, L, SEG, PRED, D, H = 4, 128, 48, 24, 192, 1024, 1024
R = B * F
EPS = 1e-15
MAXN = 1.0 - 1e-5


def norm(a):
    return np.sqrt(np.maximum(np.sum(a * a, axis=-1, keepdims=True), EPS))


def artanh(r):
    c = np.clip(r, -1.0 + 1e-7, 1.0 - 1e-7)
    return 0.5 * np.log((1.0 + c) / (1.0 - c))


def projx(a):
    n = norm(a)
    return np.where(n > MAXN, a * (MAXN / n), a)


def expmap0(v):
    n = norm(v)
    return np.tanh(n) * v / n


def mobius_add(x, y):
    x2 = np.sum(x * x, -1, keepdims=True)
    y2 = np.sum(y * y, -1, keepdims=True)
    xy = np.sum(x * y, -1, keepdims=True)
    num = (1.0 + 2.0 * xy + y2) * x + (1.0 - x2) * y
    den = 1.0 + 2.0 * xy + x2 * y2
    return num / np.maximum(den, EPS)


def draw0():
    s = mx_kscale(D)
    c = np.exp2(np.ceil(np.log2(np.sqrt(np.mean(s * s)))))
    return {"v_init": bf(np.random.standard_normal((R, D)) * 0.55 / np.sqrt(D) * s / c),
            "W_vel": bf(np.random.standard_normal((D, D)) * 1.5 / np.sqrt(D) * c / s[None, :]),
            "b_vel": bf(np.random.standard_normal(D) * 0.4 / np.sqrt(D))}


def core(v_init, W_vel, b_vel):
    x = f64(v_init)
    mx = mxq(x, 1, "e4m3") @ mxq(f64(W_vel), 1, "e4m3").T
    xn = norm(x)
    mxn = norm(mx)
    p = np.tanh(mxn / xn * artanh(xn)) * mx / mxn
    return projx(mobius_add(p, expmap0(f64(b_vel))))


def e4m3fn_bytes(y):
    return np.clip(np.asarray(y, np.float64), -448.0, 448.0).astype(np.float32).astype(ml_dtypes.float8_e4m3fn).view(np.uint8)


def e4m3fn_values(b):
    return np.asarray(b, np.uint8).view(ml_dtypes.float8_e4m3fn).astype(np.float64)


def setup_inputs():
    d = draw0()
    x0 = np.asarray(d['W_vel']).astype(np.float64)
    s = (np.max(np.abs(x0), axis=(0,), keepdims=True) / 448.0).astype(np.float32)
    out = {}
    for k, v in d.items():
        if k == 'W_vel':
            out['W_vel_bytes'] = e4m3fn_bytes(x0 / s.astype(np.float64))
            out['W_vel_scale'] = s
        else:
            out[k] = v
    return out


def reference(v_init, W_vel_bytes, W_vel_scale, b_vel):
    return core(v_init, e4m3fn_values(W_vel_bytes) * W_vel_scale.astype(np.float64), b_vel)

@@ -1,0 +1,323 @@
+from contextlib import ExitStack
+
+import concourse.mybir as mybir
+from concourse.masks import make_identity
+
+FLOPS = 2 * 512 * 1024 * 1024
+
+F32 = mybir.dt.float32
+BF16 = mybir.dt.bfloat16
+U32 = mybir.dt.uint32
+U8 = mybir.dt.uint8
+FP8 = mybir.dt.float8_e4m3fn
+FP8X4 = mybir.dt.float8_e4m3fn_x4
+ALU = mybir.AluOpType
+ACT = mybir.ActivationFunctionType
+
+P = 128
+ROWS = 512
+K = 1024
+N = 1024
+RT = ROWS // P
+WT = N // P
+G = K // 512
+EPS = 1e-15
+CMAX = 1.0 - 1e-7
+MAXN = 1.0 - 1e-5
+KF = 0.5 / (MAXN * MAXN)
+BIG = 1.0 / EPS
+
+
+def tile_directnodecomphyperbolicforecaster_pa_kernel(tc, v_init, W_vel_bytes, W_vel_scale, b_vel, out):
+    nc = tc.nc
+    with ExitStack() as ctx:
+        keep = ctx.enter_context(tc.tile_pool(name="keep", bufs=1))
+        byt = ctx.enter_context(tc.tile_pool(name="byt", bufs=1))
+        work = ctx.enter_context(tc.tile_pool(name="work", bufs=2))
+        outp = ctx.enter_context(tc.tile_pool(name="outp", bufs=4))
+        psum = ctx.enter_context(tc.psum_pool(name="psum", bufs=4))
+
+        scl = keep.tile([P, K], F32, name="scl")
+        b8 = keep.tile([P, 8], BF16, name="b8")
+        bb = keep.tile([P, N], BF16, name="bb")
+        wby = []
+        for j in range(WT):
+            t = byt.tile([P, K], U8, name="wby%d" % j)
+            wby.append(t)
+        xin = []
+        for i in range(RT):
+            t = keep.tile([P, K], BF16, name="xin%d" % i)
+            xin.append(t)
+        xg = keep.tile([P, G, ROWS, 4], BF16, name="xg", align_bytes=64)
+        wg = keep.tile([P, G, N, 4], BF16, name="wg", align_bytes=64)
+        xc = keep.tile([P, G, ROWS], U32, name="xc", align_bytes=64)
+        xsc = keep.tile([P, G, ROWS], U8, name="xsc", align_bytes=64)
+        wc = keep.tile([P, G, N], U32, name="wc", align_bytes=64)
+        wsc = keep.tile([P, G, N], U8, name="wsc", align_bytes=64)
+        xgw = xg[:].bitcast(F32)
+        wgw = wg[:].bitcast(F32)
+        one = keep.tile([P, 1], F32, name="one")
+        warm = keep.tile([P, 1], F32, name="warm")
+        ident = keep.tile([P, P], F32, name="ident")
+        s5 = keep.tile([P, 5], F32, name="s5")
+        smp = keep.tile([P, 2, RT], F32, name="smp")
+        dp = keep.tile([P, 2, RT], F32, name="dp")
+
+        def small(name, w=4):
+            return keep.tile([P, w], F32, name=name)
+
+        def load_x(i):
+            nc.sync.dma_start(out=xin[i][:], in_=v_init[P * i : P * (i + 1), :])
+
+        def load_w(j):
+            nc.sync.dma_start(out=wby[j][:], in_=W_vel_bytes[P * j : P * (j + 1), :])
+
+        banks = {}
+
+        def turn(key, src, tag):
+            words = src[:].bitcast(F32)
+            bank = psum.tile([P, G, 2, P], F32, tag=tag, name="t" + key)
+            for g in range(G):
+                for u in range(2):
+                    nc.tensor.transpose(bank[:, g, u, :], words[:, 256 * g + u : 256 * (g + 1) : 2], ident[:])
+            banks[key] = bank
+
+        def copy_out(eng, key, dst_words, col0):
+            src = banks[key][:].rearrange("p g u n -> p g n u")
+            dst = dst_words[:, :, col0 : col0 + P, :]
+            if eng == "v":
+                nc.vector.tensor_copy(out=dst, in_=src)
+            else:
+                nc.scalar.copy(out=dst, in_=src)
+
+        wbs = {}
+
+        def widen(j):
+            wb = keep.tile([P, K], BF16, name="wb%d" % j)
+            step = 512 if j == 0 else K
+            for c0 in range(0, K, step):
+                nc.vector.tensor_tensor(
+                    out=wb[:, c0 : c0 + step], in0=wby[j][:, c0 : c0 + step].bitcast(FP8), in1=scl[:, c0 : c0 + step], op=ALU.mult
+                )
+            wbs[j] = wb
+
+        def quant_x(g):
+            nc.vector.quantize_mx(
+                out=xc[:, g, :].bitcast(FP8X4), scales=xsc[:, g, :],
+                in_=xg[:, g, :, :].rearrange("p n t -> p (n t)"),
+            )
+
+        def quant_w(q):
+            for g in range(G):
+                nc.vector.quantize_mx(
+                    out=wc[:, g, 256 * q : 256 * (q + 1)].bitcast(FP8X4),
+                    scales=wsc[:, g, 256 * q : 256 * (q + 1)],
+                    in_=wg[:, g, 256 * q : 256 * (q + 1), :].rearrange("p n t -> p (n t)"),
+                )
+
+        mx = {}
+
+        def mult(q):
+            h = q // 2
+            for r in range(RT):
+                if q % 2 == 0:
+                    mx[(r, h)] = psum.tile([P, 512], F32, tag=("pa" if h == 0 else "pb"), name="mx%d_%d" % (r, h))
+                for g in range(G):
+                    nc.tensor.matmul_mx(
+                        out=mx[(r, h)][:, 256 * (q % 2) : 256 * (q % 2 + 1)],
+                        lhsT=xc[:, g, P * r : P * (r + 1)].bitcast(FP8X4),
+                        lhsT_scale=xsc[:, g, P * r : P * (r + 1)],
+                        rhs=wc[:, g, 256 * q : 256 * (q + 1)].bitcast(FP8X4),
+                        rhs_scale=wsc[:, g, 256 * q : 256 * (q + 1)],
+                        start=(g == 0),
+                        stop=(g == G - 1),
+                    )
+
+        def xnorm(i):
+            junk = work.tile([P, K], BF16, name="junkx")
+            nc.scalar.activation(out=junk[:], in_=xin[i][:], func=ACT.Square, accum_out=s5[:, i : i + 1])
+
+        def square(r, h):
+            js = work.tile([P, 512], BF16, name="junks")
+            nc.scalar.activation(out=js[:], in_=mx[(r, h)][:], func=ACT.Square, accum_out=smp[:, h, r : r + 1])
+
+        def dot(r, h):
+            jv = work.tile([P, 512], F32, name="junkv")
+            nc.vector.scalar_tensor_tensor(
+                out=jv[:], in0=mx[(r, h)][:], scalar=1.0, in1=bb[:, 512 * h : 512 * (h + 1)],
+                op0=ALU.mult, op1=ALU.mult, accum_out=dp[:, h, r : r + 1],
+            )
+
+        def vts(o, i0, s1, s2, op0, op1=None):
+            if op1 is None:
+                nc.vector.tensor_scalar(out=o, in0=i0, scalar1=s1, scalar2=None, op0=op0)
+            else:
+                nc.vector.tensor_scalar(out=o, in0=i0, scalar1=s1, scalar2=s2, op0=op0, op1=op1)
+
+        def vtt(o, i0, i1, op):
+            nc.vector.tensor_tensor(out=o, in0=i0, in1=i1, op=op)
+
+        def vstt(o, i0, s, i1, op0, op1):
+            nc.vector.scalar_tensor_tensor(out=o, in0=i0, scalar=s, in1=i1, op0=op0, op1=op1)
+
+        def gts(o, i0, s1, s2, op0, op1):
+            nc.gpsimd.tensor_scalar(out=o, in0=i0, scalar1=s1, scalar2=s2, op0=op0, op1=op1)
+
+        def gtt(o, i0, i1, op):
+            nc.gpsimd.tensor_tensor(out=o, in0=i0, in1=i1, op=op)
+
+        s8 = keep.tile([P, 8], F32, name="s8")
+        nc.scalar.dma_start(out=s8[:].rearrange("p (g t) -> p g t", t=4), in_=W_vel_scale.rearrange("o (g p t) -> p (o g) t", p=P, t=4))
+        nc.scalar.dma_start(out=b8[:], in_=b_vel.rearrange("(p c) -> p c", c=8))
+        load_w(0)
+        load_w(1)
+        for i in range(RT):
+            load_x(i)
+        for j in range(2, WT):
+            load_w(j)
+        nc.sync.dma_start(out=bb[:], in_=b_vel.partition_broadcast(P))
+
+        nc.gpsimd.memset(one[:], 1.0)
+        make_identity(nc, ident[:])
+        nc.scalar.activation(out=warm[:], in_=one[:], func=ACT.Sqrt)
+
+        for h in range(2):
+            sbank = psum.tile([P, 4, P], F32, tag="pb", name="sbank%d" % h)
+            for c in range(4):
+                nc.tensor.transpose(sbank[:, c, :], s8[:, 4 * h + c : 4 * h + c + 1].to_broadcast([P, P]), ident[:])
+            nc.vector.tensor_copy(
+                out=scl[:, 512 * h : 512 * (h + 1)].rearrange("p (j c) -> p j c", c=4),
+                in_=sbank[:].rearrange("p c j -> p j c"),
+            )
+        bsq = psum.tile([P, 1], F32, tag="pa", name="bsq")
+        for c in range(8):
+            nc.tensor.matmul(out=bsq[:], lhsT=b8[:, c : c + 1].to_broadcast([P, P]), rhs=b8[:, c : c + 1], start=(c == 0), stop=(c == 7))
+        nc.vector.tensor_copy(out=s5[:, 4:5], in_=bsq[:])
+
+        widen(0)
+        widen(1)
+        for i in range(RT):
+            turn("x%d" % i, xin[i], "pa")
+            copy_out("s", "x%d" % i, xgw, P * i)
+        quant_x(0)
+        quant_x(1)
+        for q in range(4):
+            for j in (2 * q, 2 * q + 1):
+                if j not in wbs:
+                    widen(j)
+                turn("w%d" % j, wbs[j], "pb")
+                copy_out("s", "w%d" % j, wgw, P * j)
+            quant_w(q)
+            if q < 2:
+                mult(q)
+        mult(2)
+        mult(3)
+
+        for i in range(RT):
+            xnorm(i)
+
+        n5 = small("n5", 5)
+        vts(n5[:], s5[:], EPS, None, ALU.max)
+        r5 = small("r5", 5)
+        nc.scalar.activation(out=r5[:], in_=n5[:], func=ACT.Sqrt)
+        i5 = small("i5", 5)
+        nc.vector.reciprocal(out=i5[:], in_=r5[:])
+        num = small("num")
+        vts(num[:], r5[:, 0:4], CMAX, 1.0, ALU.min, ALU.add)
+        cm1 = small("cm1")
+        vts(cm1[:], r5[:, 0:4], CMAX, 1.0, ALU.min, ALU.subtract)
+        rd = small("rd")
+        nc.vector.reciprocal(out=rd[:], in_=cm1[:])
+        base = small("base")
+        vstt(base[:], num[:], -1.0, rd[:], ALU.mult, ALU.mult)
+        lnb = small("lnb")
+        nc.scalar.activation(out=lnb[:], in_=base[:], func=ACT.Ln)
+        k2p = small("k2p")
+        vtt(k2p[:], lnb[:], i5[:, 0:4], ALU.mult)
+        lnk = small("lnk")
+        nc.scalar.activation(out=lnk[:], in_=k2p[:], func=ACT.Ln, scale=0.5)
+        kap = small("kap", 1)
+        vstt(kap[:], s5[:, 4:5], i5[:, 4:5], i5[:, 4:5], ALU.mult, ALU.mult)
+
+        for r in range(RT):
+            square(r, 0)
+            dot(r, 0)
+        for r in range(RT):
+            square(r, 1)
+
+        mn2 = small("mn2")
+        vstt(mn2[:], smp[:, 0, :], EPS, smp[:, 1, :], ALU.max, ALU.add)
+        lm = small("lm")
+        tb = small("tb", 1)
+        lz = small("lz")
+        z = small("z")
+        rm = small("rm")
+        th = small("th")
+        with tc.manual_schedule(engines={mybir.EngineType.Activation}):
+            nc.scalar.activation(out=lm[:], in_=mn2[:], func=ACT.Ln)
+            nc.scalar.activation(out=tb[:], in_=r5[:, 4:5], func=ACT.Tanh)
+            vstt(lz[:], lm[:], 0.5, lnk[:], ALU.mult, ALU.add)
+            nc.scalar.activation(out=z[:], in_=lz[:], func=ACT.Exp)
+            nc.scalar.activation(out=rm[:], in_=lm[:], func=ACT.Exp, scale=-0.5)
+            nc.scalar.activation(out=th[:], in_=z[:], func=ACT.Tanh)
+        qs2 = small("qs2", 1)
+        vts(qs2[:], tb[:], i5[:, 4:5], 2.0, ALU.mult, ALU.mult)
+        q2 = small("q2", 1)
+        vstt(q2[:], tb[:], kap[:], tb[:], ALU.mult, ALU.mult)
+        kqs = small("kqs", 1)
+        vts(kqs[:], tb[:], i5[:, 4:5], KF, ALU.mult, ALU.mult)
+        nkqs = small("nkqs", 1)
+        vts(nkqs[:], tb[:], i5[:, 4:5], -KF, ALU.mult, ALU.mult)
+        q2p1 = small("q2p1", 1)
+        vts(q2p1[:], q2[:], 1.0, None, ALU.add)
+        for r in range(RT):
+            dot(r, 1)
+        db = small("db")
+        vtt(db[:], dp[:, 0, :], dp[:, 1, :], ALU.add)
+        e1 = small("e1")
+        vtt(e1[:], rm[:], db[:], ALU.mult)
+
+        pe = small("pe")
+        vstt(pe[:], th[:], qs2[:], e1[:], ALU.mult, ALU.mult)
+        t2 = small("t2")
+        vtt(t2[:], th[:], th[:], ALU.mult)
+        prm = small("prm")
+        vstt(prm[:], th[:], KF, rm[:], ALU.mult, ALU.mult)
+        pe1 = small("pe1")
+        vts(pe1[:], pe[:], 1.0, None, ALU.add)
+        c2q = small("c2q")
+        vts(c2q[:], t2[:], nkqs[:], kqs[:], ALU.mult, ALU.add)
+        w = small("w")
+        vstt(w[:], t2[:], q2[:], pe[:], ALU.add, ALU.add)
+        den0 = small("den0")
+        vstt(den0[:], t2[:], q2[:], pe1[:], ALU.mult, ALU.add)
+        ac = small("ac")
+        vstt(ac[:], pe[:], q2p1[:], prm[:], ALU.add, ALU.mult)
+        rr = small("rr")
+        nc.vector.reciprocal(out=rr[:], in_=den0[:])
+        g0 = small("g0")
+        vstt(g0[:], den0[:], 1.5 / KF, w[:], ALU.mult, ALU.subtract)
+        b0 = small("b0")
+        vstt(b0[:], rr[:], BIG, c2q[:], ALU.min, ALU.mult)
+        f1 = small("f1")
+        vstt(f1[:], rr[:], BIG, g0[:], ALU.min, ALU.mult)
+        a0 = small("a0")
+        vstt(a0[:], rr[:], BIG, ac[:], ALU.min, ALU.mult)
+        fb = small("fb")
+        vstt(fb[:], f1[:], 1.0 / KF, b0[:], ALU.min, ALU.mult)
+        fa = small("fa")
+        vstt(fa[:], f1[:], 1.0 / KF, a0[:], ALU.min, ALU.mult)
+
+        for r in range(RT):
+            for h in range(2):
+                bq = outp.tile([P, 512], F32, name="bq")
+                bslice = bb[:, 512 * h : 512 * (h + 1)]
+                if r == 0 and h == 0:
+                    vts(bq[:], bslice, fb[:, r : r + 1], None, ALU.mult)
+                elif h == 0:
+                    nc.scalar.activation(out=bq[:], in_=bslice, func=ACT.Copy, scale=fb[:, r : r + 1])
+                else:
+                    gts(bq[:], bslice, fb[:, r : r + 1], 0.0, ALU.mult, ALU.add)
+                o = outp.tile([P, 512], F32, name="o")
+                vstt(o[:], mx[(r, h)][:], fa[:, r : r + 1], bq[:], ALU.mult, ALU.add)
+                nc.sync.dma_start(out=out[P * r : P * (r + 1), 512 * h : 512 * (h + 1)], in_=o[:])

@@ -34,8 +34,9 @@ def tile_directnodecomphyperbolicforecaster_pa_kernel(tc, v_init, W_vel_bytes, W
         keep = ctx.enter_context(tc.tile_pool(name="keep", bufs=1))
         byt = ctx.enter_context(tc.tile_pool(name="byt", bufs=1))
         work = ctx.enter_context(tc.tile_pool(name="work", bufs=2))
-        outp = ctx.enter_context(tc.tile_pool(name="outp", bufs=4))
-        psum = ctx.enter_context(tc.psum_pool(name="psum", bufs=4))
+        outp = ctx.enter_context(tc.tile_pool(name="outp", bufs=8))
+        psum = ctx.enter_context(tc.psum_pool(name="psum", bufs=1))
+        ctx.enter_context(tc.manual_schedule())
 
         scl = keep.tile([P, K], F32, name="scl")
         b8 = keep.tile([P, 8], BF16, name="b8")
@@ -59,12 +60,16 @@ def tile_directnodecomphyperbolicforecaster_pa_kernel(tc, v_init, W_vel_bytes, W
         one = keep.tile([P, 1], F32, name="one")
         warm = keep.tile([P, 1], F32, name="warm")
         ident = keep.tile([P, P], F32, name="ident")
-        s5 = keep.tile([P, 5], F32, name="s5")
-        smp = keep.tile([P, 2, RT], F32, name="smp")
-        dp = keep.tile([P, 2, RT], F32, name="dp")
+        s8 = keep.tile([P, 8], F32, name="s8")
+        sx = keep.tile([P, RT + 1], F32, name="sx")
+        smp = keep.tile([P, 3, RT], F32, name="smp")
+        dp = keep.tile([P, 3, RT], F32, name="dp")
 
         def small(name, w=4):
             return keep.tile([P, w], F32, name=name)
+
+        def bank(i, shape, name):
+            return psum.tile(shape, F32, tag="b%d" % i, name=name)
 
         def load_x(i):
             nc.sync.dma_start(out=xin[i][:], in_=v_init[P * i : P * (i + 1), :])
@@ -74,32 +79,43 @@ def tile_directnodecomphyperbolicforecaster_pa_kernel(tc, v_init, W_vel_bytes, W
 
         banks = {}
 
-        def turn(key, src, tag):
+        def turn(key, src, i):
             words = src[:].bitcast(F32)
-            bank = psum.tile([P, G, 2, P], F32, tag=tag, name="t" + key)
+            t = bank(i, [P, G, 2, P], "t" + key)
             for g in range(G):
                 for u in range(2):
-                    nc.tensor.transpose(bank[:, g, u, :], words[:, 256 * g + u : 256 * (g + 1) : 2], ident[:])
-            banks[key] = bank
+                    nc.tensor.transpose(t[:, g, u, :], words[:, 256 * g + u : 256 * (g + 1) : 2], ident[:])
+            banks[key] = t
 
-        def copy_out(eng, key, dst_words, col0):
-            src = banks[key][:].rearrange("p g u n -> p g n u")
-            dst = dst_words[:, :, col0 : col0 + P, :]
-            if eng == "v":
-                nc.vector.tensor_copy(out=dst, in_=src)
-            else:
-                nc.scalar.copy(out=dst, in_=src)
+        def copy_out(key, dst_words, col0):
+            nc.scalar.copy(out=dst_words[:, :, col0 : col0 + P, :], in_=banks[key][:].rearrange("p g u n -> p g n u"))
+
+        def spread(h):
+            t = bank(4 + h, [P, 4, P], "sbank%d" % h)
+            for c in range(4):
+                nc.tensor.transpose(t[:, c, :], s8[:, 4 * h + c : 4 * h + c + 1].to_broadcast([P, P]), ident[:])
+            nc.scalar.copy(
+                out=scl[:, 512 * h : 512 * (h + 1)].rearrange("p (j c) -> p j c", c=4),
+                in_=t[:].rearrange("p c j -> p j c"),
+            )
 
         wbs = {}
 
-        def widen(j):
+        def widen(j, step=K):
             wb = keep.tile([P, K], BF16, name="wb%d" % j)
-            step = 512 if j == 0 else K
             for c0 in range(0, K, step):
                 nc.vector.tensor_tensor(
                     out=wb[:, c0 : c0 + step], in0=wby[j][:, c0 : c0 + step].bitcast(FP8), in1=scl[:, c0 : c0 + step], op=ALU.mult
                 )
             wbs[j] = wb
+
+        def w_turn(j):
+            turn("w%d" % j, wbs[j], 4 + j % 4)
+            copy_out("w%d" % j, wgw, P * j)
+
+        def x_turn(i):
+            turn("x%d" % i, xin[i], i)
+            copy_out("x%d" % i, xgw, P * i)
 
         def quant_x(g):
             nc.vector.quantize_mx(
@@ -118,13 +134,20 @@ def tile_directnodecomphyperbolicforecaster_pa_kernel(tc, v_init, W_vel_bytes, W
         mx = {}
 
         def mult(q):
-            h = q // 2
             for r in range(RT):
-                if q % 2 == 0:
-                    mx[(r, h)] = psum.tile([P, 512], F32, tag=("pa" if h == 0 else "pb"), name="mx%d_%d" % (r, h))
+                if q == 0:
+                    t = bank(r, [P, 512], "mxa%d" % r)
+                    mx[(0, r)] = t[:, :]
+                    mx[("q0", r)] = t[:, 0:256]
+                    mx[("q1", r)] = t[:, 256:512]
+                if q >= 2 and r % 2 == 0:
+                    t = bank(2 * q + r // 2, [P, 512], "mxb%d_%d" % (q, r))
+                    mx[(q - 1, r)] = t[:, 0:256]
+                    mx[(q - 1, r + 1)] = t[:, 256:512]
+                dst = mx[("q%d" % q, r)] if q < 2 else mx[(q - 1, r)]
                 for g in range(G):
                     nc.tensor.matmul_mx(
-                        out=mx[(r, h)][:, 256 * (q % 2) : 256 * (q % 2 + 1)],
+                        out=dst,
                         lhsT=xc[:, g, P * r : P * (r + 1)].bitcast(FP8X4),
                         lhsT_scale=xsc[:, g, P * r : P * (r + 1)],
                         rhs=wc[:, g, 256 * q : 256 * (q + 1)].bitcast(FP8X4),
@@ -133,19 +156,40 @@ def tile_directnodecomphyperbolicforecaster_pa_kernel(tc, v_init, W_vel_bytes, W
                         stop=(g == G - 1),
                     )
 
-        def xnorm(i):
-            junk = work.tile([P, K], BF16, name="junkx")
-            nc.scalar.activation(out=junk[:], in_=xin[i][:], func=ACT.Square, accum_out=s5[:, i : i + 1])
+        COLS = {0: (0, 512), 1: (512, 768), 2: (768, 1024)}
 
-        def square(r, h):
+        def xnorm_vector(i):
+            junk = keep.tile([P, K], F32, name="junkx")
+            nc.vector.scalar_tensor_tensor(
+                out=junk[:], in0=xin[i][:], scalar=1.0, in1=xin[i][:], op0=ALU.mult, op1=ALU.mult, accum_out=sx[:, i : i + 1],
+            )
+
+        grams = {}
+
+        def gram(i):
+            t = bank(i, [P, P], "gram%d" % i)
+            for s in range(4 * G):
+                xt = xg[:, s // 4, P * i : P * (i + 1), s % 4]
+                nc.tensor.matmul(out=t[:], lhsT=xt, rhs=xt, start=(s == 0), stop=(s == 4 * G - 1))
+            grams[i] = t
+
+        def diag(i):
+            jd = work.tile([P, P], F32, name="junkd")
+            nc.vector.scalar_tensor_tensor(
+                out=jd[:], in0=grams[i][:], scalar=1.0, in1=ident[:], op0=ALU.mult, op1=ALU.mult, accum_out=sx[:, i : i + 1],
+            )
+
+        def square(c, r):
+            w = COLS[c][1] - COLS[c][0]
             js = work.tile([P, 512], BF16, name="junks")
-            nc.scalar.activation(out=js[:], in_=mx[(r, h)][:], func=ACT.Square, accum_out=smp[:, h, r : r + 1])
+            nc.scalar.activation(out=js[:, 0:w], in_=mx[(c, r)], func=ACT.Square, accum_out=smp[:, c, r : r + 1])
 
-        def dot(r, h):
+        def dot(c, r):
+            w = COLS[c][1] - COLS[c][0]
             jv = work.tile([P, 512], F32, name="junkv")
             nc.vector.scalar_tensor_tensor(
-                out=jv[:], in0=mx[(r, h)][:], scalar=1.0, in1=bb[:, 512 * h : 512 * (h + 1)],
-                op0=ALU.mult, op1=ALU.mult, accum_out=dp[:, h, r : r + 1],
+                out=jv[:, 0:w], in0=mx[(c, r)], scalar=1.0, in1=bb[:, COLS[c][0] : COLS[c][1]],
+                op0=ALU.mult, op1=ALU.mult, accum_out=dp[:, c, r : r + 1],
             )
 
         def vts(o, i0, s1, s2, op0, op1=None):
@@ -160,19 +204,14 @@ def tile_directnodecomphyperbolicforecaster_pa_kernel(tc, v_init, W_vel_bytes, W
         def vstt(o, i0, s, i1, op0, op1):
             nc.vector.scalar_tensor_tensor(out=o, in0=i0, scalar=s, in1=i1, op0=op0, op1=op1)
 
-        def gts(o, i0, s1, s2, op0, op1):
-            nc.gpsimd.tensor_scalar(out=o, in0=i0, scalar1=s1, scalar2=s2, op0=op0, op1=op1)
-
-        def gtt(o, i0, i1, op):
-            nc.gpsimd.tensor_tensor(out=o, in0=i0, in1=i1, op=op)
-
-        s8 = keep.tile([P, 8], F32, name="s8")
         nc.scalar.dma_start(out=s8[:].rearrange("p (g t) -> p g t", t=4), in_=W_vel_scale.rearrange("o (g p t) -> p (o g) t", p=P, t=4))
         nc.scalar.dma_start(out=b8[:], in_=b_vel.rearrange("(p c) -> p c", c=8))
+        load_x(0)
         load_w(0)
+        load_x(1)
         load_w(1)
-        for i in range(RT):
-            load_x(i)
+        load_x(2)
+        load_x(3)
         for j in range(2, WT):
             load_w(j)
         nc.sync.dma_start(out=bb[:], in_=b_vel.partition_broadcast(P))
@@ -181,108 +220,127 @@ def tile_directnodecomphyperbolicforecaster_pa_kernel(tc, v_init, W_vel_bytes, W
         make_identity(nc, ident[:])
         nc.scalar.activation(out=warm[:], in_=one[:], func=ACT.Sqrt)
 
-        for h in range(2):
-            sbank = psum.tile([P, 4, P], F32, tag="pb", name="sbank%d" % h)
-            for c in range(4):
-                nc.tensor.transpose(sbank[:, c, :], s8[:, 4 * h + c : 4 * h + c + 1].to_broadcast([P, P]), ident[:])
-            nc.vector.tensor_copy(
-                out=scl[:, 512 * h : 512 * (h + 1)].rearrange("p (j c) -> p j c", c=4),
-                in_=sbank[:].rearrange("p c j -> p j c"),
-            )
-        bsq = psum.tile([P, 1], F32, tag="pa", name="bsq")
+        xnorm_vector(0)
+        spread(0)
+        spread(1)
+        bsq = bank(6, [P, 1], "bsq")
         for c in range(8):
             nc.tensor.matmul(out=bsq[:], lhsT=b8[:, c : c + 1].to_broadcast([P, P]), rhs=b8[:, c : c + 1], start=(c == 0), stop=(c == 7))
-        nc.vector.tensor_copy(out=s5[:, 4:5], in_=bsq[:])
 
-        widen(0)
+        widen(0, 512)
+        x_turn(0)
+        x_turn(1)
+        x_turn(2)
+        w_turn(0)
         widen(1)
-        for i in range(RT):
-            turn("x%d" % i, xin[i], "pa")
-            copy_out("s", "x%d" % i, xgw, P * i)
+        nc.vector.tensor_copy(out=sx[:, RT : RT + 1], in_=bsq[:])
+        x_turn(3)
+        w_turn(1)
+        gram(1)
+        gram(2)
+        widen(2)
+        w_turn(2)
+        gram(3)
+        widen(3)
+        w_turn(3)
+        for i in range(1, RT):
+            diag(i)
+        n9 = small("n9", 9)
+        vts(n9[:, 0:5], sx[:], EPS, None, ALU.max)
+        vts(n9[:, 5:9], sx[:, 0:RT], EPS, CMAX * CMAX, ALU.max, ALU.min)
         quant_x(0)
         quant_x(1)
-        for q in range(4):
-            for j in (2 * q, 2 * q + 1):
-                if j not in wbs:
-                    widen(j)
-                turn("w%d" % j, wbs[j], "pb")
-                copy_out("s", "w%d" % j, wgw, P * j)
-            quant_w(q)
-            if q < 2:
-                mult(q)
+        quant_w(0)
+        mult(0)
+        r5 = small("r5", 5)
+        nc.scalar.activation(out=r5[:], in_=n9[:, 4:9], func=ACT.Sqrt)
+        rb = r5[:, 0:1]
+        cx = r5[:, 1:5]
+        lnn = small("lnn")
+        nc.scalar.activation(out=lnn[:], in_=n9[:, 0:4], func=ACT.Ln)
+        lnp = small("lnp")
+        nc.scalar.activation(out=lnp[:], in_=cx, func=ACT.Ln, bias=1.0)
+        lnq = small("lnq")
+        nc.scalar.activation(out=lnq[:], in_=cx, func=ACT.Ln, scale=-1.0, bias=1.0)
+        widen(4)
+        w_turn(4)
+        at2 = small("at2")
+        vtt(at2[:], lnp[:], lnq[:], ALU.subtract)
+        lna = small("lna")
+        nc.scalar.activation(out=lna[:], in_=at2[:], func=ACT.Ln, scale=0.5)
+        widen(5)
+        w_turn(5)
+        quant_w(1)
+        mult(1)
+        lnk = small("lnk")
+        vstt(lnk[:], lnn[:], -0.5, lna[:], ALU.mult, ALU.add)
+        widen(6)
+        square(0, 0)
+        w_turn(6)
+        widen(7)
+        square(0, 1)
+        w_turn(7)
+        quant_w(2)
         mult(2)
+        dot(0, 0)
+        quant_w(3)
         mult(3)
 
-        for i in range(RT):
-            xnorm(i)
-
-        n5 = small("n5", 5)
-        vts(n5[:], s5[:], EPS, None, ALU.max)
-        r5 = small("r5", 5)
-        nc.scalar.activation(out=r5[:], in_=n5[:], func=ACT.Sqrt)
-        i5 = small("i5", 5)
-        nc.vector.reciprocal(out=i5[:], in_=r5[:])
-        num = small("num")
-        vts(num[:], r5[:, 0:4], CMAX, 1.0, ALU.min, ALU.add)
-        cm1 = small("cm1")
-        vts(cm1[:], r5[:, 0:4], CMAX, 1.0, ALU.min, ALU.subtract)
-        rd = small("rd")
-        nc.vector.reciprocal(out=rd[:], in_=cm1[:])
-        base = small("base")
-        vstt(base[:], num[:], -1.0, rd[:], ALU.mult, ALU.mult)
-        lnb = small("lnb")
-        nc.scalar.activation(out=lnb[:], in_=base[:], func=ACT.Ln)
-        k2p = small("k2p")
-        vtt(k2p[:], lnb[:], i5[:, 0:4], ALU.mult)
-        lnk = small("lnk")
-        nc.scalar.activation(out=lnk[:], in_=k2p[:], func=ACT.Ln, scale=0.5)
+        square(0, 2)
+        square(0, 3)
+        for r in range(1, RT):
+            dot(0, r)
+        for r in range(RT):
+            square(1, r)
+        for r in range(RT):
+            dot(1, r)
+        a01 = small("a01")
+        vstt(a01[:], smp[:, 0, :], EPS, smp[:, 1, :], ALU.max, ALU.add)
+        d01 = small("d01")
+        vtt(d01[:], dp[:, 0, :], dp[:, 1, :], ALU.add)
+        ib = small("ib", 1)
+        nc.vector.reciprocal(out=ib[:], in_=rb)
         kap = small("kap", 1)
-        vstt(kap[:], s5[:, 4:5], i5[:, 4:5], i5[:, 4:5], ALU.mult, ALU.mult)
+        vstt(kap[:], sx[:, RT : RT + 1], ib[:], ib[:], ALU.mult, ALU.mult)
 
         for r in range(RT):
-            square(r, 0)
-            dot(r, 0)
-        for r in range(RT):
-            square(r, 1)
-
-        mn2 = small("mn2")
-        vstt(mn2[:], smp[:, 0, :], EPS, smp[:, 1, :], ALU.max, ALU.add)
+            square(2, r)
         lm = small("lm")
+        for r in range(RT):
+            nc.scalar.activation(out=lm[:, r : r + 1], in_=smp[:, 2, r : r + 1], func=ACT.Ln, bias=a01[:, r : r + 1])
         tb = small("tb", 1)
-        lz = small("lz")
-        z = small("z")
-        rm = small("rm")
+        nc.scalar.activation(out=tb[:], in_=rb, func=ACT.Tanh)
+        for r in range(RT):
+            dot(2, r)
+        lzz = small("lzz", 8)
+        vstt(lzz[:, 0:4], lm[:], 0.5, lnk[:], ALU.mult, ALU.add)
+        vts(lzz[:, 4:8], lm[:], -0.5, None, ALU.mult)
+        zz = small("zz", 8)
+        nc.scalar.activation(out=zz[:], in_=lzz[:], func=ACT.Exp)
         th = small("th")
-        with tc.manual_schedule(engines={mybir.EngineType.Activation}):
-            nc.scalar.activation(out=lm[:], in_=mn2[:], func=ACT.Ln)
-            nc.scalar.activation(out=tb[:], in_=r5[:, 4:5], func=ACT.Tanh)
-            vstt(lz[:], lm[:], 0.5, lnk[:], ALU.mult, ALU.add)
-            nc.scalar.activation(out=z[:], in_=lz[:], func=ACT.Exp)
-            nc.scalar.activation(out=rm[:], in_=lm[:], func=ACT.Exp, scale=-0.5)
-            nc.scalar.activation(out=th[:], in_=z[:], func=ACT.Tanh)
+        nc.scalar.activation(out=th[:], in_=zz[:, 0:4], func=ACT.Tanh)
+        rm = zz[:, 4:8]
         qs2 = small("qs2", 1)
-        vts(qs2[:], tb[:], i5[:, 4:5], 2.0, ALU.mult, ALU.mult)
+        vts(qs2[:], tb[:], ib[:], 2.0, ALU.mult, ALU.mult)
         q2 = small("q2", 1)
         vstt(q2[:], tb[:], kap[:], tb[:], ALU.mult, ALU.mult)
         kqs = small("kqs", 1)
-        vts(kqs[:], tb[:], i5[:, 4:5], KF, ALU.mult, ALU.mult)
+        vts(kqs[:], tb[:], ib[:], KF, ALU.mult, ALU.mult)
         nkqs = small("nkqs", 1)
-        vts(nkqs[:], tb[:], i5[:, 4:5], -KF, ALU.mult, ALU.mult)
+        vts(nkqs[:], tb[:], ib[:], -KF, ALU.mult, ALU.mult)
         q2p1 = small("q2p1", 1)
         vts(q2p1[:], q2[:], 1.0, None, ALU.add)
-        for r in range(RT):
-            dot(r, 1)
         db = small("db")
-        vtt(db[:], dp[:, 0, :], dp[:, 1, :], ALU.add)
+        vtt(db[:], d01[:], dp[:, 2, :], ALU.add)
         e1 = small("e1")
-        vtt(e1[:], rm[:], db[:], ALU.mult)
+        vtt(e1[:], rm, db[:], ALU.mult)
 
         pe = small("pe")
         vstt(pe[:], th[:], qs2[:], e1[:], ALU.mult, ALU.mult)
         t2 = small("t2")
         vtt(t2[:], th[:], th[:], ALU.mult)
         prm = small("prm")
-        vstt(prm[:], th[:], KF, rm[:], ALU.mult, ALU.mult)
+        vstt(prm[:], th[:], KF, rm, ALU.mult, ALU.mult)
         pe1 = small("pe1")
         vts(pe1[:], pe[:], 1.0, None, ALU.add)
         c2q = small("c2q")
@@ -308,16 +366,18 @@ def tile_directnodecomphyperbolicforecaster_pa_kernel(tc, v_init, W_vel_bytes, W
         fa = small("fa")
         vstt(fa[:], f1[:], 1.0 / KF, a0[:], ALU.min, ALU.mult)
 
-        for r in range(RT):
-            for h in range(2):
+        for h in range(2):
+            for r in range(RT):
                 bq = outp.tile([P, 512], F32, name="bq")
                 bslice = bb[:, 512 * h : 512 * (h + 1)]
                 if r == 0 and h == 0:
                     vts(bq[:], bslice, fb[:, r : r + 1], None, ALU.mult)
-                elif h == 0:
-                    nc.scalar.activation(out=bq[:], in_=bslice, func=ACT.Copy, scale=fb[:, r : r + 1])
                 else:
-                    gts(bq[:], bslice, fb[:, r : r + 1], 0.0, ALU.mult, ALU.add)
+                    nc.scalar.activation(out=bq[:], in_=bslice, func=ACT.Copy, scale=fb[:, r : r + 1])
                 o = outp.tile([P, 512], F32, name="o")
-                vstt(o[:], mx[(r, h)][:], fa[:, r : r + 1], bq[:], ALU.mult, ALU.add)
+                if h == 0:
+                    vstt(o[:], mx[(0, r)], fa[:, r : r + 1], bq[:], ALU.mult, ALU.add)
+                else:
+                    vstt(o[:, 0:256], mx[(1, r)], fa[:, r : r + 1], bq[:, 0:256], ALU.mult, ALU.add)
+                    vstt(o[:, 256:512], mx[(2, r)], fa[:, r : r + 1], bq[:, 256:512], ALU.mult, ALU.add)
                 nc.sync.dma_start(out=out[P * r : P * (r + 1), 512 * h : 512 * (h + 1)], in_=o[:])

@@ -50,11 +50,11 @@ def tile_directnodecomphyperbolicforecaster_pa_kernel(tc, v_init, W_vel_bytes, W
             t = keep.tile([P, K], BF16, name="xin%d" % i)
             xin.append(t)
         xg = keep.tile([P, G, ROWS, 4], BF16, name="xg", align_bytes=64)
-        wg = keep.tile([P, G, N, 4], BF16, name="wg", align_bytes=64)
+        wg = keep.tile([P, 4, G, 256, 4], BF16, name="wg", align_bytes=64)
         xc = keep.tile([P, G, ROWS], U32, name="xc", align_bytes=64)
         xsc = keep.tile([P, G, ROWS], U8, name="xsc", align_bytes=64)
-        wc = keep.tile([P, G, N], U32, name="wc", align_bytes=64)
-        wsc = keep.tile([P, G, N], U8, name="wsc", align_bytes=64)
+        wc = keep.tile([P, 4, G, 256], U32, name="wc", align_bytes=64)
+        wsc = keep.tile([P, 4, G, 256], U8, name="wsc", align_bytes=64)
         xgw = xg[:].bitcast(F32)
         wgw = wg[:].bitcast(F32)
         one = keep.tile([P, 1], F32, name="one")
@@ -87,8 +87,8 @@ def tile_directnodecomphyperbolicforecaster_pa_kernel(tc, v_init, W_vel_bytes, W
                     nc.tensor.transpose(t[:, g, u, :], words[:, 256 * g + u : 256 * (g + 1) : 2], ident[:])
             banks[key] = t
 
-        def copy_out(key, dst_words, col0):
-            nc.scalar.copy(out=dst_words[:, :, col0 : col0 + P, :], in_=banks[key][:].rearrange("p g u n -> p g n u"))
+        def copy_out(key, dst_words):
+            nc.scalar.copy(out=dst_words, in_=banks[key][:].rearrange("p g u n -> p g n u"))
 
         def spread(h):
             t = bank(4 + h, [P, 4, P], "sbank%d" % h)
@@ -111,25 +111,24 @@ def tile_directnodecomphyperbolicforecaster_pa_kernel(tc, v_init, W_vel_bytes, W
 
         def w_turn(j):
             turn("w%d" % j, wbs[j], 4 + j % 4)
-            copy_out("w%d" % j, wgw, P * j)
+            copy_out("w%d" % j, wgw[:, j // 2, :, P * (j % 2) : P * (j % 2 + 1), :])
 
         def x_turn(i):
             turn("x%d" % i, xin[i], i)
-            copy_out("x%d" % i, xgw, P * i)
+            copy_out("x%d" % i, xgw[:, :, P * i : P * (i + 1), :])
 
-        def quant_x(g):
+        def quant_x():
             nc.vector.quantize_mx(
-                out=xc[:, g, :].bitcast(FP8X4), scales=xsc[:, g, :],
-                in_=xg[:, g, :, :].rearrange("p n t -> p (n t)"),
+                out=xc[:].rearrange("p g n -> p (g n)").bitcast(FP8X4), scales=xsc[:].rearrange("p g n -> p (g n)"),
+                in_=xg[:].rearrange("p g n t -> p (g n t)"),
             )
 
         def quant_w(q):
-            for g in range(G):
-                nc.vector.quantize_mx(
-                    out=wc[:, g, 256 * q : 256 * (q + 1)].bitcast(FP8X4),
-                    scales=wsc[:, g, 256 * q : 256 * (q + 1)],
-                    in_=wg[:, g, 256 * q : 256 * (q + 1), :].rearrange("p n t -> p (n t)"),
-                )
+            nc.vector.quantize_mx(
+                out=wc[:, q, :, :].rearrange("p g n -> p (g n)").bitcast(FP8X4),
+                scales=wsc[:, q, :, :].rearrange("p g n -> p (g n)"),
+                in_=wg[:, q, :, :, :].rearrange("p g n t -> p (g n t)"),
+            )
 
         mx = {}
 
@@ -150,8 +149,8 @@ def tile_directnodecomphyperbolicforecaster_pa_kernel(tc, v_init, W_vel_bytes, W
                         out=dst,
                         lhsT=xc[:, g, P * r : P * (r + 1)].bitcast(FP8X4),
                         lhsT_scale=xsc[:, g, P * r : P * (r + 1)],
-                        rhs=wc[:, g, 256 * q : 256 * (q + 1)].bitcast(FP8X4),
-                        rhs_scale=wsc[:, g, 256 * q : 256 * (q + 1)],
+                        rhs=wc[:, q, g, :].bitcast(FP8X4),
+                        rhs_scale=wsc[:, q, g, :],
                         start=(g == 0),
                         stop=(g == G - 1),
                     )
@@ -164,20 +163,9 @@ def tile_directnodecomphyperbolicforecaster_pa_kernel(tc, v_init, W_vel_bytes, W
                 out=junk[:], in0=xin[i][:], scalar=1.0, in1=xin[i][:], op0=ALU.mult, op1=ALU.mult, accum_out=sx[:, i : i + 1],
             )
 
-        grams = {}
-
-        def gram(i):
-            t = bank(i, [P, P], "gram%d" % i)
-            for s in range(4 * G):
-                xt = xg[:, s // 4, P * i : P * (i + 1), s % 4]
-                nc.tensor.matmul(out=t[:], lhsT=xt, rhs=xt, start=(s == 0), stop=(s == 4 * G - 1))
-            grams[i] = t
-
-        def diag(i):
-            jd = work.tile([P, P], F32, name="junkd")
-            nc.vector.scalar_tensor_tensor(
-                out=jd[:], in0=grams[i][:], scalar=1.0, in1=ident[:], op0=ALU.mult, op1=ALU.mult, accum_out=sx[:, i : i + 1],
-            )
+        def xnorm_scalar(i):
+            junk = work.tile([P, K], BF16, name="junkh")
+            nc.scalar.activation(out=junk[:], in_=xin[i][:], func=ACT.Square, accum_out=sx[:, i : i + 1])
 
         def square(c, r):
             w = COLS[c][1] - COLS[c][0]
@@ -236,22 +224,21 @@ def tile_directnodecomphyperbolicforecaster_pa_kernel(tc, v_init, W_vel_bytes, W
         nc.vector.tensor_copy(out=sx[:, RT : RT + 1], in_=bsq[:])
         x_turn(3)
         w_turn(1)
-        gram(1)
-        gram(2)
+        xnorm_scalar(1)
         widen(2)
         w_turn(2)
-        gram(3)
+        xnorm_scalar(2)
         widen(3)
         w_turn(3)
-        for i in range(1, RT):
-            diag(i)
+        xnorm_scalar(3)
+        quant_x()
+        quant_w(0)
+        mult(0)
+        widen(4)
+        w_turn(4)
         n9 = small("n9", 9)
         vts(n9[:, 0:5], sx[:], EPS, None, ALU.max)
         vts(n9[:, 5:9], sx[:, 0:RT], EPS, CMAX * CMAX, ALU.max, ALU.min)
-        quant_x(0)
-        quant_x(1)
-        quant_w(0)
-        mult(0)
         r5 = small("r5", 5)
         nc.scalar.activation(out=r5[:], in_=n9[:, 4:9], func=ACT.Sqrt)
         rb = r5[:, 0:1]
@@ -262,18 +249,14 @@ def tile_directnodecomphyperbolicforecaster_pa_kernel(tc, v_init, W_vel_bytes, W
         nc.scalar.activation(out=lnp[:], in_=cx, func=ACT.Ln, bias=1.0)
         lnq = small("lnq")
         nc.scalar.activation(out=lnq[:], in_=cx, func=ACT.Ln, scale=-1.0, bias=1.0)
-        widen(4)
-        w_turn(4)
-        at2 = small("at2")
-        vtt(at2[:], lnp[:], lnq[:], ALU.subtract)
-        lna = small("lna")
-        nc.scalar.activation(out=lna[:], in_=at2[:], func=ACT.Ln, scale=0.5)
         widen(5)
         w_turn(5)
         quant_w(1)
         mult(1)
-        lnk = small("lnk")
-        vstt(lnk[:], lnn[:], -0.5, lna[:], ALU.mult, ALU.add)
+        at2 = small("at2")
+        vtt(at2[:], lnp[:], lnq[:], ALU.subtract)
+        lna = small("lna")
+        nc.scalar.activation(out=lna[:], in_=at2[:], func=ACT.Ln, scale=0.5)
         widen(6)
         square(0, 0)
         w_turn(6)
@@ -283,6 +266,8 @@ def tile_directnodecomphyperbolicforecaster_pa_kernel(tc, v_init, W_vel_bytes, W
         quant_w(2)
         mult(2)
         dot(0, 0)
+        lnk = small("lnk")
+        vstt(lnk[:], lnn[:], -0.5, lna[:], ALU.mult, ALU.add)
         quant_w(3)
         mult(3)
 
@@ -296,12 +281,6 @@ def tile_directnodecomphyperbolicforecaster_pa_kernel(tc, v_init, W_vel_bytes, W
             dot(1, r)
         a01 = small("a01")
         vstt(a01[:], smp[:, 0, :], EPS, smp[:, 1, :], ALU.max, ALU.add)
-        d01 = small("d01")
-        vtt(d01[:], dp[:, 0, :], dp[:, 1, :], ALU.add)
-        ib = small("ib", 1)
-        nc.vector.reciprocal(out=ib[:], in_=rb)
-        kap = small("kap", 1)
-        vstt(kap[:], sx[:, RT : RT + 1], ib[:], ib[:], ALU.mult, ALU.mult)
 
         for r in range(RT):
             square(2, r)
@@ -312,59 +291,46 @@ def tile_directnodecomphyperbolicforecaster_pa_kernel(tc, v_init, W_vel_bytes, W
         nc.scalar.activation(out=tb[:], in_=rb, func=ACT.Tanh)
         for r in range(RT):
             dot(2, r)
+        ib = small("ib", 1)
+        nc.vector.reciprocal(out=ib[:], in_=rb)
         lzz = small("lzz", 8)
         vstt(lzz[:, 0:4], lm[:], 0.5, lnk[:], ALU.mult, ALU.add)
         vts(lzz[:, 4:8], lm[:], -0.5, None, ALU.mult)
-        zz = small("zz", 8)
-        nc.scalar.activation(out=zz[:], in_=lzz[:], func=ACT.Exp)
-        th = small("th")
-        nc.scalar.activation(out=th[:], in_=zz[:, 0:4], func=ACT.Tanh)
-        rm = zz[:, 4:8]
-        qs2 = small("qs2", 1)
-        vts(qs2[:], tb[:], ib[:], 2.0, ALU.mult, ALU.mult)
+        row = small("row", 16)
+        nc.scalar.activation(out=row[:, 0:8], in_=lzz[:], func=ACT.Exp)
+        nc.scalar.activation(out=row[:, 8:12], in_=row[:, 0:4], func=ACT.Tanh)
+        ntb = small("ntb", 1)
+        vts(ntb[:], tb[:], ib[:], -1.0, ALU.mult, ALU.mult)
         q2 = small("q2", 1)
-        vstt(q2[:], tb[:], kap[:], tb[:], ALU.mult, ALU.mult)
-        kqs = small("kqs", 1)
-        vts(kqs[:], tb[:], ib[:], KF, ALU.mult, ALU.mult)
-        nkqs = small("nkqs", 1)
-        vts(nkqs[:], tb[:], ib[:], -KF, ALU.mult, ALU.mult)
-        q2p1 = small("q2p1", 1)
-        vts(q2p1[:], q2[:], 1.0, None, ALU.add)
+        vstt(q2[:], ntb[:], ntb[:], sx[:, RT : RT + 1], ALU.mult, ALU.mult)
+        kq = small("kq", 1)
+        vts(kq[:], q2[:], -1.0, KF, ALU.add, ALU.mult)
         db = small("db")
-        vtt(db[:], d01[:], dp[:, 2, :], ALU.add)
-        e1 = small("e1")
-        vtt(e1[:], rm, db[:], ALU.mult)
+        nc.vector.tensor_reduce(out=db[:], in_=dp[:].rearrange("p c r -> p r c"), axis=mybir.AxisListType.X, op=ALU.add)
+        vstt(row[:, 12:16], db[:], ntb[:], row[:, 4:8], ALU.mult, ALU.mult)
 
-        pe = small("pe")
-        vstt(pe[:], th[:], qs2[:], e1[:], ALU.mult, ALU.mult)
-        t2 = small("t2")
-        vtt(t2[:], th[:], th[:], ALU.mult)
-        prm = small("prm")
-        vstt(prm[:], th[:], KF, rm, ALU.mult, ALU.mult)
+        l1 = keep.tile([P, 3, RT], F32, name="l1")
+        vtt(l1[:], row[:, 8:12].unsqueeze(1).to_broadcast([P, 3, RT]), row[:, 4:16].rearrange("p (a r) -> p a r", a=3), ALU.mult)
+        alpha = l1[:, 0, :]
+        t2 = l1[:, 1, :]
+        u3 = keep.tile([P, 3, RT], F32, name="u3")
         pe1 = small("pe1")
-        vts(pe1[:], pe[:], 1.0, None, ALU.add)
-        c2q = small("c2q")
-        vts(c2q[:], t2[:], nkqs[:], kqs[:], ALU.mult, ALU.add)
-        w = small("w")
-        vstt(w[:], t2[:], q2[:], pe[:], ALU.add, ALU.add)
+        vts(pe1[:], l1[:, 2, :], -2.0, 1.0, ALU.mult, ALU.add)
+        vts(u3[:, 1, :], t2, -1.0, ntb[:], ALU.add, ALU.mult)
+        omq = small("omq")
+        vts(omq[:], t2, -1.0, kq[:], ALU.add, ALU.mult)
         den0 = small("den0")
-        vstt(den0[:], t2[:], q2[:], pe1[:], ALU.mult, ALU.add)
-        ac = small("ac")
-        vstt(ac[:], pe[:], q2p1[:], prm[:], ALU.add, ALU.mult)
+        vstt(den0[:], t2, q2[:], pe1[:], ALU.mult, ALU.add)
+        vstt(u3[:, 2, :], pe1[:], q2[:], alpha, ALU.add, ALU.mult)
+        vstt(u3[:, 0, :], den0[:], 1.5 - KF, omq[:], ALU.mult, ALU.add)
         rr = small("rr")
         nc.vector.reciprocal(out=rr[:], in_=den0[:])
-        g0 = small("g0")
-        vstt(g0[:], den0[:], 1.5 / KF, w[:], ALU.mult, ALU.subtract)
-        b0 = small("b0")
-        vstt(b0[:], rr[:], BIG, c2q[:], ALU.min, ALU.mult)
-        f1 = small("f1")
-        vstt(f1[:], rr[:], BIG, g0[:], ALU.min, ALU.mult)
-        a0 = small("a0")
-        vstt(a0[:], rr[:], BIG, ac[:], ALU.min, ALU.mult)
-        fb = small("fb")
-        vstt(fb[:], f1[:], 1.0 / KF, b0[:], ALU.min, ALU.mult)
-        fa = small("fa")
-        vstt(fa[:], f1[:], 1.0 / KF, a0[:], ALU.min, ALU.mult)
+        v3 = keep.tile([P, 3, RT], F32, name="v3")
+        vstt(v3[:], rr[:].unsqueeze(1).to_broadcast([P, 3, RT]), BIG, u3[:], ALU.min, ALU.mult)
+        ff = keep.tile([P, 2, RT], F32, name="ff")
+        vstt(ff[:], v3[:, 0:1, :].to_broadcast([P, 2, RT]), 1.0, v3[:, 1:3, :], ALU.min, ALU.mult)
+        fb = ff[:, 0, :]
+        fa = ff[:, 1, :]
 
         for h in range(2):
             for r in range(RT):

@@ -61,6 +61,9 @@ def tile_directnodecomphyperbolicforecaster_pa_kernel(tc, v_init, W_vel_bytes, W
         warm = keep.tile([P, 1], F32, name="warm")
         ident = keep.tile([P, P], F32, name="ident")
         s8 = keep.tile([P, 8], F32, name="s8")
+        ones = keep.tile([P, P], F32, name="ones")
+        pb = keep.tile([P, 1], F32, name="pb")
+        half = keep.tile([P, 5], F32, name="half")
         sx = keep.tile([P, RT + 1], F32, name="sx")
         smp = keep.tile([P, 3, RT], F32, name="smp")
         dp = keep.tile([P, 3, RT], F32, name="dp")
@@ -94,7 +97,8 @@ def tile_directnodecomphyperbolicforecaster_pa_kernel(tc, v_init, W_vel_bytes, W
             t = bank(4 + h, [P, 4, P], "sbank%d" % h)
             for c in range(4):
                 nc.tensor.transpose(t[:, c, :], s8[:, 4 * h + c : 4 * h + c + 1].to_broadcast([P, P]), ident[:])
-            nc.scalar.copy(
+            copy = nc.vector.tensor_copy if h == 0 else nc.scalar.copy
+            copy(
                 out=scl[:, 512 * h : 512 * (h + 1)].rearrange("p (j c) -> p j c", c=4),
                 in_=t[:].rearrange("p c j -> p j c"),
             )
@@ -206,14 +210,18 @@ def tile_directnodecomphyperbolicforecaster_pa_kernel(tc, v_init, W_vel_bytes, W
 
         nc.gpsimd.memset(one[:], 1.0)
         make_identity(nc, ident[:])
-        nc.scalar.activation(out=warm[:], in_=one[:], func=ACT.Sqrt)
+        nc.gpsimd.memset(ones[:], 1.0)
+        nc.gpsimd.memset(half[:], 0.5)
+        nc.scalar.activation(out=warm[:], in_=one[:], func=ACT.Ln)
 
         xnorm_vector(0)
+        jb = small("jb", 8)
+        nc.scalar.activation(out=jb[:], in_=b8[:], func=ACT.Square, accum_out=pb[:])
         spread(0)
         spread(1)
         bsq = bank(6, [P, 1], "bsq")
-        for c in range(8):
-            nc.tensor.matmul(out=bsq[:], lhsT=b8[:, c : c + 1].to_broadcast([P, P]), rhs=b8[:, c : c + 1], start=(c == 0), stop=(c == 7))
+        nc.tensor.matmul(out=bsq[:], lhsT=ones[:], rhs=pb[:], start=True, stop=True)
+        nc.scalar.copy(out=sx[:, RT : RT + 1], in_=bsq[:])
 
         widen(0, 512)
         x_turn(0)
@@ -221,7 +229,6 @@ def tile_directnodecomphyperbolicforecaster_pa_kernel(tc, v_init, W_vel_bytes, W
         x_turn(2)
         w_turn(0)
         widen(1)
-        nc.vector.tensor_copy(out=sx[:, RT : RT + 1], in_=bsq[:])
         x_turn(3)
         w_turn(1)
         xnorm_scalar(1)
@@ -236,43 +243,41 @@ def tile_directnodecomphyperbolicforecaster_pa_kernel(tc, v_init, W_vel_bytes, W
         mult(0)
         widen(4)
         w_turn(4)
+        widen(5)
+        w_turn(5)
         n9 = small("n9", 9)
         vts(n9[:, 0:5], sx[:], EPS, None, ALU.max)
         vts(n9[:, 5:9], sx[:, 0:RT], EPS, CMAX * CMAX, ALU.max, ALU.min)
         r5 = small("r5", 5)
-        nc.scalar.activation(out=r5[:], in_=n9[:, 4:9], func=ACT.Sqrt)
+        nc.gpsimd.tensor_tensor(out=r5[:], in0=n9[:, 4:9], in1=half[:], op=ALU.pow)
         rb = r5[:, 0:1]
         cx = r5[:, 1:5]
         lnn = small("lnn")
         nc.scalar.activation(out=lnn[:], in_=n9[:, 0:4], func=ACT.Ln)
+        quant_w(1)
+        mult(1)
+        widen(6)
+        w_turn(6)
         lnp = small("lnp")
         nc.scalar.activation(out=lnp[:], in_=cx, func=ACT.Ln, bias=1.0)
         lnq = small("lnq")
         nc.scalar.activation(out=lnq[:], in_=cx, func=ACT.Ln, scale=-1.0, bias=1.0)
-        widen(5)
-        w_turn(5)
-        quant_w(1)
-        mult(1)
-        at2 = small("at2")
-        vtt(at2[:], lnp[:], lnq[:], ALU.subtract)
-        lna = small("lna")
-        nc.scalar.activation(out=lna[:], in_=at2[:], func=ACT.Ln, scale=0.5)
-        widen(6)
-        square(0, 0)
-        w_turn(6)
         widen(7)
-        square(0, 1)
         w_turn(7)
         quant_w(2)
         mult(2)
         dot(0, 0)
-        lnk = small("lnk")
-        vstt(lnk[:], lnn[:], -0.5, lna[:], ALU.mult, ALU.add)
+        at2 = small("at2")
+        vtt(at2[:], lnp[:], lnq[:], ALU.subtract)
+        lna = small("lna")
+        nc.scalar.activation(out=lna[:], in_=at2[:], func=ACT.Ln, scale=0.5)
         quant_w(3)
         mult(3)
+        lnk = small("lnk")
+        vstt(lnk[:], lnn[:], -0.5, lna[:], ALU.mult, ALU.add)
 
-        square(0, 2)
-        square(0, 3)
+        for r in range(RT):
+            square(0, r)
         for r in range(1, RT):
             dot(0, r)
         for r in range(RT):
@@ -293,11 +298,11 @@ def tile_directnodecomphyperbolicforecaster_pa_kernel(tc, v_init, W_vel_bytes, W
             dot(2, r)
         ib = small("ib", 1)
         nc.vector.reciprocal(out=ib[:], in_=rb)
-        lzz = small("lzz", 8)
-        vstt(lzz[:, 0:4], lm[:], 0.5, lnk[:], ALU.mult, ALU.add)
-        vts(lzz[:, 4:8], lm[:], -0.5, None, ALU.mult)
+        lz = small("lz")
+        vstt(lz[:], lm[:], 0.5, lnk[:], ALU.mult, ALU.add)
         row = small("row", 16)
-        nc.scalar.activation(out=row[:, 0:8], in_=lzz[:], func=ACT.Exp)
+        nc.scalar.activation(out=row[:, 4:8], in_=lm[:], func=ACT.Exp, scale=-0.5)
+        nc.scalar.activation(out=row[:, 0:4], in_=lz[:], func=ACT.Exp)
         nc.scalar.activation(out=row[:, 8:12], in_=row[:, 0:4], func=ACT.Tanh)
         ntb = small("ntb", 1)
         vts(ntb[:], tb[:], ib[:], -1.0, ALU.mult, ALU.mult)

@@ -262,11 +262,14 @@ def tile_directnodecomphyperbolicforecaster_pa_kernel(tc, v_init, W_vel_bytes, W
         nc.scalar.activation(out=lnp[:], in_=cx, func=ACT.Ln, bias=1.0)
         lnq = small("lnq")
         nc.scalar.activation(out=lnq[:], in_=cx, func=ACT.Ln, scale=-1.0, bias=1.0)
+        row = small("row", 28)
+        nc.scalar.copy(out=row[:, 20:21], in_=rb)
         widen(7)
         w_turn(7)
         quant_w(2)
         mult(2)
         dot(0, 0)
+        dot(0, 1)
         at2 = small("at2")
         vtt(at2[:], lnp[:], lnq[:], ALU.subtract)
         lna = small("lna")
@@ -276,9 +279,12 @@ def tile_directnodecomphyperbolicforecaster_pa_kernel(tc, v_init, W_vel_bytes, W
         lnk = small("lnk")
         vstt(lnk[:], lnn[:], -0.5, lna[:], ALU.mult, ALU.add)
 
+        ib = small("ib", 1)
+        nc.vector.reciprocal(out=ib[:], in_=rb)
+
         for r in range(RT):
             square(0, r)
-        for r in range(1, RT):
+        for r in range(2, RT):
             dot(0, r)
         for r in range(RT):
             square(1, r)
@@ -292,36 +298,32 @@ def tile_directnodecomphyperbolicforecaster_pa_kernel(tc, v_init, W_vel_bytes, W
         lm = small("lm")
         for r in range(RT):
             nc.scalar.activation(out=lm[:, r : r + 1], in_=smp[:, 2, r : r + 1], func=ACT.Ln, bias=a01[:, r : r + 1])
-        tb = small("tb", 1)
-        nc.scalar.activation(out=tb[:], in_=rb, func=ACT.Tanh)
         for r in range(RT):
             dot(2, r)
-        ib = small("ib", 1)
-        nc.vector.reciprocal(out=ib[:], in_=rb)
-        lz = small("lz")
-        vstt(lz[:], lm[:], 0.5, lnk[:], ALU.mult, ALU.add)
-        row = small("row", 16)
-        nc.scalar.activation(out=row[:, 4:8], in_=lm[:], func=ACT.Exp, scale=-0.5)
-        nc.scalar.activation(out=row[:, 0:4], in_=lz[:], func=ACT.Exp)
-        nc.scalar.activation(out=row[:, 8:12], in_=row[:, 0:4], func=ACT.Tanh)
-        ntb = small("ntb", 1)
-        vts(ntb[:], tb[:], ib[:], -1.0, ALU.mult, ALU.mult)
+        lzz = small("lzz", 8)
+        vts(lzz[:, 0:4], lm[:], -0.5, None, ALU.mult)
+        vstt(lzz[:, 4:8], lm[:], 0.5, lnk[:], ALU.mult, ALU.add)
+        nc.scalar.activation(out=row[:, 4:28].rearrange("p (a c) -> p a c", a=2)[:, :, 0:4], in_=lzz[:].rearrange("p (a c) -> p a c", a=2), func=ACT.Exp)
+        nc.scalar.activation(out=row[:, 8:13], in_=row[:, 16:21], func=ACT.Tanh)
+        tb = row[:, 12:13]
+        beta = small("beta", 1)
+        nc.scalar.activation(out=beta[:], in_=tb, func=ACT.Copy, scale=ib[:])
         q2 = small("q2", 1)
-        vstt(q2[:], ntb[:], ntb[:], sx[:, RT : RT + 1], ALU.mult, ALU.mult)
+        nc.scalar.activation(out=q2[:], in_=tb, func=ACT.Square)
         kq = small("kq", 1)
-        vts(kq[:], q2[:], -1.0, KF, ALU.add, ALU.mult)
+        nc.scalar.activation(out=kq[:], in_=q2[:], func=ACT.Copy, scale=KF, bias=-KF)
         db = small("db")
         nc.vector.tensor_reduce(out=db[:], in_=dp[:].rearrange("p c r -> p r c"), axis=mybir.AxisListType.X, op=ALU.add)
-        vstt(row[:, 12:16], db[:], ntb[:], row[:, 4:8], ALU.mult, ALU.mult)
+        vstt(row[:, 0:4], row[:, 4:8], 2.0, db[:], ALU.mult, ALU.mult)
 
         l1 = keep.tile([P, 3, RT], F32, name="l1")
-        vtt(l1[:], row[:, 8:12].unsqueeze(1).to_broadcast([P, 3, RT]), row[:, 4:16].rearrange("p (a r) -> p a r", a=3), ALU.mult)
-        alpha = l1[:, 0, :]
-        t2 = l1[:, 1, :]
+        vtt(l1[:], row[:, 8:12].unsqueeze(1).to_broadcast([P, 3, RT]), row[:, 0:12].rearrange("p (a r) -> p a r", a=3), ALU.mult)
+        alpha = l1[:, 1, :]
+        t2 = l1[:, 2, :]
         u3 = keep.tile([P, 3, RT], F32, name="u3")
         pe1 = small("pe1")
-        vts(pe1[:], l1[:, 2, :], -2.0, 1.0, ALU.mult, ALU.add)
-        vts(u3[:, 1, :], t2, -1.0, ntb[:], ALU.add, ALU.mult)
+        vts(pe1[:], l1[:, 0, :], beta[:], 1.0, ALU.mult, ALU.add)
+        vts(u3[:, 1, :], t2, -1.0, beta[:], ALU.add, ALU.mult)
         omq = small("omq")
         vts(omq[:], t2, -1.0, kq[:], ALU.add, ALU.mult)
         den0 = small("den0")
@@ -334,21 +336,27 @@ def tile_directnodecomphyperbolicforecaster_pa_kernel(tc, v_init, W_vel_bytes, W
         vstt(v3[:], rr[:].unsqueeze(1).to_broadcast([P, 3, RT]), BIG, u3[:], ALU.min, ALU.mult)
         ff = keep.tile([P, 2, RT], F32, name="ff")
         vstt(ff[:], v3[:, 0:1, :].to_broadcast([P, 2, RT]), 1.0, v3[:, 1:3, :], ALU.min, ALU.mult)
-        fb = ff[:, 0, :]
+        nfb = ff[:, 0, :]
         fa = ff[:, 1, :]
 
-        for h in range(2):
-            for r in range(RT):
-                bq = outp.tile([P, 512], F32, name="bq")
-                bslice = bb[:, 512 * h : 512 * (h + 1)]
-                if r == 0 and h == 0:
-                    vts(bq[:], bslice, fb[:, r : r + 1], None, ALU.mult)
+        ORDER = [(1, 0), (2, 0), (0, 0), (0, 1), (0, 2), (0, 3), (1, 1), (2, 1), (1, 2), (2, 2), (1, 3), (2, 3)]
+        bqs = {}
+        outs = {}
+        for c, r in ORDER:
+            c0, c1 = COLS[c]
+            h = 0 if c == 0 else 1
+            if (h, r) not in outs:
+                t = outp.tile([P, 512], F32, name="bq")
+                bqs[(h, r)] = t
+                t = outp.tile([P, 512], F32, name="o")
+                outs[(h, r)] = t
+                if (c, r) == ORDER[0]:
+                    vts(bqs[(h, r)][:, 0:256], bb[:, c0:c1], nfb[:, r : r + 1], None, ALU.mult)
+                    nc.scalar.activation(out=bqs[(h, r)][:, 256:512], in_=bb[:, 768:1024], func=ACT.Copy, scale=nfb[:, r : r + 1])
                 else:
-                    nc.scalar.activation(out=bq[:], in_=bslice, func=ACT.Copy, scale=fb[:, r : r + 1])
-                o = outp.tile([P, 512], F32, name="o")
-                if h == 0:
-                    vstt(o[:], mx[(0, r)], fa[:, r : r + 1], bq[:], ALU.mult, ALU.add)
-                else:
-                    vstt(o[:, 0:256], mx[(1, r)], fa[:, r : r + 1], bq[:, 0:256], ALU.mult, ALU.add)
-                    vstt(o[:, 256:512], mx[(2, r)], fa[:, r : r + 1], bq[:, 256:512], ALU.mult, ALU.add)
-                nc.sync.dma_start(out=out[P * r : P * (r + 1), 512 * h : 512 * (h + 1)], in_=o[:])
+                    nc.scalar.activation(out=bqs[(h, r)][:], in_=bb[:, 512 * h : 512 * (h + 1)], func=ACT.Copy, scale=nfb[:, r : r + 1])
+            lo = c0 - 512 * h
+            hi = c1 - 512 * h
+            vstt(outs[(h, r)][:, lo:hi], mx[(c, r)], fa[:, r : r + 1], bqs[(h, r)][:, lo:hi], ALU.mult, ALU.subtract)
+            if c != 1:
+                nc.sync.dma_start(out=out[P * r : P * (r + 1), 512 * h : 512 * (h + 1)], in_=outs[(h, r)][:])

@@ -239,52 +239,39 @@ def tile_directnodecomphyperbolicforecaster_pa_kernel(tc, v_init, W_vel_bytes, W
         w_turn(3)
         xnorm_scalar(3)
         quant_x()
-        quant_w(0)
-        mult(0)
         widen(4)
         w_turn(4)
         widen(5)
         w_turn(5)
+        widen(6)
+        w_turn(6)
+        widen(7)
+        w_turn(7)
         n9 = small("n9", 9)
         vts(n9[:, 0:5], sx[:], EPS, None, ALU.max)
         vts(n9[:, 5:9], sx[:, 0:RT], EPS, CMAX * CMAX, ALU.max, ALU.min)
-        r5 = small("r5", 5)
-        nc.gpsimd.tensor_tensor(out=r5[:], in0=n9[:, 4:9], in1=half[:], op=ALU.pow)
-        rb = r5[:, 0:1]
-        cx = r5[:, 1:5]
-        lnn = small("lnn")
-        nc.scalar.activation(out=lnn[:], in_=n9[:, 0:4], func=ACT.Ln)
+        row = small("row", 28)
+        nc.gpsimd.tensor_tensor(out=row[:, 20:25], in0=n9[:, 4:9], in1=half[:], op=ALU.pow)
+        rb = row[:, 20:21]
+        cx = row[:, 21:25]
+        quant_w(0)
+        mult(0)
         quant_w(1)
         mult(1)
-        widen(6)
-        w_turn(6)
+        quant_w(2)
+        mult(2)
+        quant_w(3)
+        mult(3)
+
+        for r in range(RT):
+            square(0, r)
+        lnn = small("lnn")
+        nc.scalar.activation(out=lnn[:], in_=n9[:, 0:4], func=ACT.Ln)
         lnp = small("lnp")
         nc.scalar.activation(out=lnp[:], in_=cx, func=ACT.Ln, bias=1.0)
         lnq = small("lnq")
         nc.scalar.activation(out=lnq[:], in_=cx, func=ACT.Ln, scale=-1.0, bias=1.0)
-        row = small("row", 28)
-        nc.scalar.copy(out=row[:, 20:21], in_=rb)
-        widen(7)
-        w_turn(7)
-        quant_w(2)
-        mult(2)
-        dot(0, 0)
-        dot(0, 1)
-        at2 = small("at2")
-        vtt(at2[:], lnp[:], lnq[:], ALU.subtract)
-        lna = small("lna")
-        nc.scalar.activation(out=lna[:], in_=at2[:], func=ACT.Ln, scale=0.5)
-        quant_w(3)
-        mult(3)
-        lnk = small("lnk")
-        vstt(lnk[:], lnn[:], -0.5, lna[:], ALU.mult, ALU.add)
-
-        ib = small("ib", 1)
-        nc.vector.reciprocal(out=ib[:], in_=rb)
-
         for r in range(RT):
-            square(0, r)
-        for r in range(2, RT):
             dot(0, r)
         for r in range(RT):
             square(1, r)
@@ -292,14 +279,22 @@ def tile_directnodecomphyperbolicforecaster_pa_kernel(tc, v_init, W_vel_bytes, W
             dot(1, r)
         a01 = small("a01")
         vstt(a01[:], smp[:, 0, :], EPS, smp[:, 1, :], ALU.max, ALU.add)
+        at2 = small("at2")
+        vtt(at2[:], lnp[:], lnq[:], ALU.subtract)
+        ib = small("ib", 1)
+        nc.vector.reciprocal(out=ib[:], in_=rb)
 
         for r in range(RT):
             square(2, r)
+        lna = small("lna")
+        nc.scalar.activation(out=lna[:], in_=at2[:], func=ACT.Ln, scale=0.5)
         lm = small("lm")
         for r in range(RT):
             nc.scalar.activation(out=lm[:, r : r + 1], in_=smp[:, 2, r : r + 1], func=ACT.Ln, bias=a01[:, r : r + 1])
         for r in range(RT):
             dot(2, r)
+        lnk = small("lnk")
+        vstt(lnk[:], lnn[:], -0.5, lna[:], ALU.mult, ALU.add)
         lzz = small("lzz", 8)
         vts(lzz[:, 0:4], lm[:], -0.5, None, ALU.mult)
         vstt(lzz[:, 4:8], lm[:], 0.5, lnk[:], ALU.mult, ALU.add)

@@ -38,7 +38,6 @@ def tile_directnodecomphyperbolicforecaster_pa_kernel(tc, v_init, W_vel_bytes, W
         psum = ctx.enter_context(tc.psum_pool(name="psum", bufs=1))
         ctx.enter_context(tc.manual_schedule())
 
-        scl = keep.tile([P, K], F32, name="scl")
         b8 = keep.tile([P, 8], BF16, name="b8")
         bb = keep.tile([P, N], BF16, name="bb")
         wby = []
@@ -56,7 +55,6 @@ def tile_directnodecomphyperbolicforecaster_pa_kernel(tc, v_init, W_vel_bytes, W
         wc = keep.tile([P, 4, G, 256], U32, name="wc", align_bytes=64)
         wsc = keep.tile([P, 4, G, 256], U8, name="wsc", align_bytes=64)
         xgw = xg[:].bitcast(F32)
-        wgw = wg[:].bitcast(F32)
         one = keep.tile([P, 1], F32, name="one")
         warm = keep.tile([P, 1], F32, name="warm")
         ident = keep.tile([P, P], F32, name="ident")
@@ -64,9 +62,10 @@ def tile_directnodecomphyperbolicforecaster_pa_kernel(tc, v_init, W_vel_bytes, W
         ones = keep.tile([P, P], F32, name="ones")
         pb = keep.tile([P, 1], F32, name="pb")
         half = keep.tile([P, 5], F32, name="half")
+        nhalf = keep.tile([P, 5], F32, name="nhalf")
         sx = keep.tile([P, RT + 1], F32, name="sx")
-        smp = keep.tile([P, 3, RT], F32, name="smp")
-        dp = keep.tile([P, 3, RT], F32, name="dp")
+        smp = keep.tile([P, 2, RT], F32, name="smp")
+        dp = keep.tile([P, 2, RT], F32, name="dp")
 
         def small(name, w=4):
             return keep.tile([P, w], F32, name=name)
@@ -82,44 +81,40 @@ def tile_directnodecomphyperbolicforecaster_pa_kernel(tc, v_init, W_vel_bytes, W
 
         banks = {}
 
-        def turn(key, src, i):
-            words = src[:].bitcast(F32)
-            t = bank(i, [P, G, 2, P], "t" + key)
+        wb = []
+        for j in range(WT):
+            t = keep.tile([P, K], BF16, name="wb%d" % j)
+            wb.append(t)
+
+        def cast(engine, j, c0, c1):
+            engine.tensor_copy(out=wb[j][:, c0:c1], in_=wby[j][:, c0:c1].bitcast(FP8))
+
+        def w_turn(q, g):
+            t = bank(4 + (2 * q + g) % 4, [P, 2, 2, P], "tw%d_%d" % (q, g))
+            for jj in range(2):
+                words = wb[2 * q + jj][:].bitcast(F32)
+                for u in range(2):
+                    nc.tensor.transpose(t[:, u, jj, :], words[:, 256 * g + u : 256 * (g + 1) : 2], ident[:])
+            banks[("w", q, g)] = t
+
+        def w_exit(q, g):
+            nc.vector.tensor_tensor(
+                out=wg[:, q, g, :, :].rearrange("p n (u e) -> p n u e", e=2),
+                in0=banks[("w", q, g)][:].rearrange("p u j n -> p u (j n)").bitcast(BF16).rearrange("p u (n e) -> p n u e", e=2),
+                in1=s8[:, 4 * g : 4 * g + 4].rearrange("p (u e) -> p u e", e=2).unsqueeze(1).to_broadcast([P, 256, 2, 2]),
+                op=ALU.mult,
+            )
+
+        def x_turn(i):
+            words = xin[i][:].bitcast(F32)
+            t = bank(i, [P, G, 2, P], "tx%d" % i)
             for g in range(G):
                 for u in range(2):
                     nc.tensor.transpose(t[:, g, u, :], words[:, 256 * g + u : 256 * (g + 1) : 2], ident[:])
-            banks[key] = t
+            banks[("x", i)] = t
 
-        def copy_out(key, dst_words):
-            nc.scalar.copy(out=dst_words, in_=banks[key][:].rearrange("p g u n -> p g n u"))
-
-        def spread(h):
-            t = bank(4 + h, [P, 4, P], "sbank%d" % h)
-            for c in range(4):
-                nc.tensor.transpose(t[:, c, :], s8[:, 4 * h + c : 4 * h + c + 1].to_broadcast([P, P]), ident[:])
-            copy = nc.vector.tensor_copy if h == 0 else nc.scalar.copy
-            copy(
-                out=scl[:, 512 * h : 512 * (h + 1)].rearrange("p (j c) -> p j c", c=4),
-                in_=t[:].rearrange("p c j -> p j c"),
-            )
-
-        wbs = {}
-
-        def widen(j, step=K):
-            wb = keep.tile([P, K], BF16, name="wb%d" % j)
-            for c0 in range(0, K, step):
-                nc.vector.tensor_tensor(
-                    out=wb[:, c0 : c0 + step], in0=wby[j][:, c0 : c0 + step].bitcast(FP8), in1=scl[:, c0 : c0 + step], op=ALU.mult
-                )
-            wbs[j] = wb
-
-        def w_turn(j):
-            turn("w%d" % j, wbs[j], 4 + j % 4)
-            copy_out("w%d" % j, wgw[:, j // 2, :, P * (j % 2) : P * (j % 2 + 1), :])
-
-        def x_turn(i):
-            turn("x%d" % i, xin[i], i)
-            copy_out("x%d" % i, xgw[:, :, P * i : P * (i + 1), :])
+        def x_copy(i):
+            nc.scalar.copy(out=xgw[:, :, P * i : P * (i + 1), :], in_=banks[("x", i)][:].rearrange("p g u n -> p g n u"))
 
         def quant_x():
             nc.vector.quantize_mx(
@@ -136,51 +131,33 @@ def tile_directnodecomphyperbolicforecaster_pa_kernel(tc, v_init, W_vel_bytes, W
 
         mx = {}
 
-        def mult(q):
-            for r in range(RT):
-                if q == 0:
-                    t = bank(r, [P, 512], "mxa%d" % r)
-                    mx[(0, r)] = t[:, :]
-                    mx[("q0", r)] = t[:, 0:256]
-                    mx[("q1", r)] = t[:, 256:512]
-                if q >= 2 and r % 2 == 0:
-                    t = bank(2 * q + r // 2, [P, 512], "mxb%d_%d" % (q, r))
-                    mx[(q - 1, r)] = t[:, 0:256]
-                    mx[(q - 1, r + 1)] = t[:, 256:512]
-                dst = mx[("q%d" % q, r)] if q < 2 else mx[(q - 1, r)]
-                for g in range(G):
-                    nc.tensor.matmul_mx(
-                        out=dst,
-                        lhsT=xc[:, g, P * r : P * (r + 1)].bitcast(FP8X4),
-                        lhsT_scale=xsc[:, g, P * r : P * (r + 1)],
-                        rhs=wc[:, q, g, :].bitcast(FP8X4),
-                        rhs_scale=wsc[:, q, g, :],
-                        start=(g == 0),
-                        stop=(g == G - 1),
-                    )
+        def mult(q, r):
+            c = q // 2
+            if q % 2 == 0:
+                mx[(c, r)] = bank(4 * c + r, [P, 512], "mx%d_%d" % (c, r))
+            for g in range(G):
+                nc.tensor.matmul_mx(
+                    out=mx[(c, r)][:, 256 * (q % 2) : 256 * (q % 2 + 1)],
+                    lhsT=xc[:, g, P * r : P * (r + 1)].bitcast(FP8X4),
+                    lhsT_scale=xsc[:, g, P * r : P * (r + 1)],
+                    rhs=wc[:, q, g, :].bitcast(FP8X4),
+                    rhs_scale=wsc[:, q, g, :],
+                    start=(g == 0),
+                    stop=(g == G - 1),
+                )
 
-        COLS = {0: (0, 512), 1: (512, 768), 2: (768, 1024)}
-
-        def xnorm_vector(i):
-            junk = keep.tile([P, K], F32, name="junkx")
-            nc.vector.scalar_tensor_tensor(
-                out=junk[:], in0=xin[i][:], scalar=1.0, in1=xin[i][:], op0=ALU.mult, op1=ALU.mult, accum_out=sx[:, i : i + 1],
-            )
-
-        def xnorm_scalar(i):
+        def xnorm(i):
             junk = work.tile([P, K], BF16, name="junkh")
             nc.scalar.activation(out=junk[:], in_=xin[i][:], func=ACT.Square, accum_out=sx[:, i : i + 1])
 
         def square(c, r):
-            w = COLS[c][1] - COLS[c][0]
             js = work.tile([P, 512], BF16, name="junks")
-            nc.scalar.activation(out=js[:, 0:w], in_=mx[(c, r)], func=ACT.Square, accum_out=smp[:, c, r : r + 1])
+            nc.scalar.activation(out=js[:], in_=mx[(c, r)][:], func=ACT.Square, accum_out=smp[:, c, r : r + 1])
 
         def dot(c, r):
-            w = COLS[c][1] - COLS[c][0]
             jv = work.tile([P, 512], F32, name="junkv")
             nc.vector.scalar_tensor_tensor(
-                out=jv[:, 0:w], in0=mx[(c, r)], scalar=1.0, in1=bb[:, COLS[c][0] : COLS[c][1]],
+                out=jv[:], in0=mx[(c, r)][:], scalar=1.0, in1=bb[:, 512 * c : 512 * (c + 1)],
                 op0=ALU.mult, op1=ALU.mult, accum_out=dp[:, c, r : r + 1],
             )
 
@@ -198,111 +175,125 @@ def tile_directnodecomphyperbolicforecaster_pa_kernel(tc, v_init, W_vel_bytes, W
 
         nc.scalar.dma_start(out=s8[:].rearrange("p (g t) -> p g t", t=4), in_=W_vel_scale.rearrange("o (g p t) -> p (o g) t", p=P, t=4))
         nc.scalar.dma_start(out=b8[:], in_=b_vel.rearrange("(p c) -> p c", c=8))
-        load_x(0)
         load_w(0)
-        load_x(1)
         load_w(1)
+        load_x(0)
+        load_w(2)
+        load_w(3)
+        load_x(1)
+        load_w(4)
         load_x(2)
+        load_w(5)
         load_x(3)
-        for j in range(2, WT):
-            load_w(j)
+        load_w(6)
+        load_w(7)
         nc.sync.dma_start(out=bb[:], in_=b_vel.partition_broadcast(P))
 
-        nc.gpsimd.memset(one[:], 1.0)
+        nc.vector.memset(one[:], 1.0)
         make_identity(nc, ident[:])
-        nc.gpsimd.memset(ones[:], 1.0)
-        nc.gpsimd.memset(half[:], 0.5)
+        nc.vector.memset(ones[:], 1.0)
+        nc.vector.memset(half[:], 0.5)
+        nc.vector.memset(nhalf[:], -0.5)
         nc.scalar.activation(out=warm[:], in_=one[:], func=ACT.Ln)
 
-        xnorm_vector(0)
         jb = small("jb", 8)
         nc.scalar.activation(out=jb[:], in_=b8[:], func=ACT.Square, accum_out=pb[:])
-        spread(0)
-        spread(1)
-        bsq = bank(6, [P, 1], "bsq")
-        nc.tensor.matmul(out=bsq[:], lhsT=ones[:], rhs=pb[:], start=True, stop=True)
-        nc.scalar.copy(out=sx[:, RT : RT + 1], in_=bsq[:])
 
-        widen(0, 512)
+        for c0 in (0, 512):
+            for j in (0, 1):
+                cast(nc.vector, j, c0, c0 + 512)
+        for j in range(2, WT):
+            cast(nc.gpsimd, j, 0, K)
+        w_turn(0, 0)
+        w_turn(0, 1)
+        bsq = bank(3, [P, 1], "bsq")
+        nc.tensor.matmul(out=bsq[:], lhsT=ones[:], rhs=pb[:], start=True, stop=True)
         x_turn(0)
         x_turn(1)
+        w_turn(1, 0)
+        w_turn(1, 1)
         x_turn(2)
-        w_turn(0)
-        widen(1)
+        xnorm(0)
+        nc.scalar.copy(out=sx[:, RT : RT + 1], in_=bsq[:])
+        x_copy(0)
+        x_copy(1)
         x_turn(3)
-        w_turn(1)
-        xnorm_scalar(1)
-        widen(2)
-        w_turn(2)
-        xnorm_scalar(2)
-        widen(3)
-        w_turn(3)
-        xnorm_scalar(3)
+        xnorm(1)
+        x_copy(2)
+        x_copy(3)
+        xnorm(2)
+        xnorm(3)
+        w_exit(0, 0)
+        w_exit(0, 1)
+        w_turn(2, 0)
+        w_turn(2, 1)
+        w_exit(1, 0)
+        w_exit(1, 1)
+        w_turn(3, 0)
+        w_turn(3, 1)
         quant_x()
-        widen(4)
-        w_turn(4)
-        widen(5)
-        w_turn(5)
-        widen(6)
-        w_turn(6)
-        widen(7)
-        w_turn(7)
+        quant_w(0)
+        w_exit(2, 0)
+        for r in range(RT):
+            mult(0, r)
+        quant_w(1)
+        for r in range(RT):
+            mult(1, r)
         n9 = small("n9", 9)
-        vts(n9[:, 0:5], sx[:], EPS, None, ALU.max)
-        vts(n9[:, 5:9], sx[:, 0:RT], EPS, CMAX * CMAX, ALU.max, ALU.min)
+        nc.gpsimd.tensor_scalar(out=n9[:, 0:5], in0=sx[:], scalar1=EPS, scalar2=None, op0=ALU.max)
+        nc.gpsimd.tensor_scalar(out=n9[:, 5:9], in0=sx[:, 0:RT], scalar1=EPS, scalar2=CMAX * CMAX, op0=ALU.max, op1=ALU.min)
         row = small("row", 28)
         nc.gpsimd.tensor_tensor(out=row[:, 20:25], in0=n9[:, 4:9], in1=half[:], op=ALU.pow)
+        ir = small("ir", 5)
+        nc.gpsimd.tensor_tensor(out=ir[:], in0=n9[:, 0:5], in1=nhalf[:], op=ALU.pow)
         rb = row[:, 20:21]
         cx = row[:, 21:25]
-        quant_w(0)
-        mult(0)
-        quant_w(1)
-        mult(1)
-        quant_w(2)
-        mult(2)
-        quant_w(3)
-        mult(3)
-
+        w_exit(2, 1)
         for r in range(RT):
             square(0, r)
-        lnn = small("lnn")
-        nc.scalar.activation(out=lnn[:], in_=n9[:, 0:4], func=ACT.Ln)
+        w_exit(3, 0)
+        quant_w(2)
+        w_exit(3, 1)
+        for r in range(RT):
+            mult(2, r)
+        dot(0, 0)
+        quant_w(3)
+        for r in range(RT):
+            mult(3, r)
+
         lnp = small("lnp")
         nc.scalar.activation(out=lnp[:], in_=cx, func=ACT.Ln, bias=1.0)
         lnq = small("lnq")
         nc.scalar.activation(out=lnq[:], in_=cx, func=ACT.Ln, scale=-1.0, bias=1.0)
-        for r in range(RT):
+        for r in range(1, RT):
             dot(0, r)
-        for r in range(RT):
-            square(1, r)
-        for r in range(RT):
-            dot(1, r)
         a01 = small("a01")
-        vstt(a01[:], smp[:, 0, :], EPS, smp[:, 1, :], ALU.max, ALU.add)
+        nc.gpsimd.tensor_scalar(out=a01[:], in0=smp[:, 0, :], scalar1=EPS, scalar2=None, op0=ALU.max)
         at2 = small("at2")
-        vtt(at2[:], lnp[:], lnq[:], ALU.subtract)
-        ib = small("ib", 1)
-        nc.vector.reciprocal(out=ib[:], in_=rb)
+        nc.gpsimd.tensor_tensor(out=at2[:], in0=lnp[:], in1=lnq[:], op=ALU.subtract)
+        kp = small("kp")
+        nc.gpsimd.tensor_tensor(out=kp[:], in0=at2[:], in1=ir[:, 0:4], op=ALU.mult)
+        ib = ir[:, 4:5]
 
         for r in range(RT):
-            square(2, r)
-        lna = small("lna")
-        nc.scalar.activation(out=lna[:], in_=at2[:], func=ACT.Ln, scale=0.5)
+            square(1, r)
+        lnk = small("lnk")
+        nc.scalar.activation(out=lnk[:], in_=kp[:], func=ACT.Ln, scale=0.5)
         lm = small("lm")
         for r in range(RT):
-            nc.scalar.activation(out=lm[:, r : r + 1], in_=smp[:, 2, r : r + 1], func=ACT.Ln, bias=a01[:, r : r + 1])
-        for r in range(RT):
-            dot(2, r)
-        lnk = small("lnk")
-        vstt(lnk[:], lnn[:], -0.5, lna[:], ALU.mult, ALU.add)
+            nc.scalar.activation(out=lm[:, r : r + 1], in_=smp[:, 1, r : r + 1], func=ACT.Ln, bias=a01[:, r : r + 1])
+        dot(1, 0)
+        dot(1, 1)
+        dot(1, 2)
         lzz = small("lzz", 8)
         vts(lzz[:, 0:4], lm[:], -0.5, None, ALU.mult)
         vstt(lzz[:, 4:8], lm[:], 0.5, lnk[:], ALU.mult, ALU.add)
+        dot(1, 3)
         nc.scalar.activation(out=row[:, 4:28].rearrange("p (a c) -> p a c", a=2)[:, :, 0:4], in_=lzz[:].rearrange("p (a c) -> p a c", a=2), func=ACT.Exp)
         nc.scalar.activation(out=row[:, 8:13], in_=row[:, 16:21], func=ACT.Tanh)
         tb = row[:, 12:13]
         beta = small("beta", 1)
-        nc.scalar.activation(out=beta[:], in_=tb, func=ACT.Copy, scale=ib[:])
+        nc.scalar.activation(out=beta[:], in_=tb, func=ACT.Copy, scale=ib)
         q2 = small("q2", 1)
         nc.scalar.activation(out=q2[:], in_=tb, func=ACT.Square)
         kq = small("kq", 1)
@@ -334,24 +325,10 @@ def tile_directnodecomphyperbolicforecaster_pa_kernel(tc, v_init, W_vel_bytes, W
         nfb = ff[:, 0, :]
         fa = ff[:, 1, :]
 
-        ORDER = [(1, 0), (2, 0), (0, 0), (0, 1), (0, 2), (0, 3), (1, 1), (2, 1), (1, 2), (2, 2), (1, 3), (2, 3)]
-        bqs = {}
-        outs = {}
+        ORDER = [(c, r) for r in range(RT) for c in range(2)]
         for c, r in ORDER:
-            c0, c1 = COLS[c]
-            h = 0 if c == 0 else 1
-            if (h, r) not in outs:
-                t = outp.tile([P, 512], F32, name="bq")
-                bqs[(h, r)] = t
-                t = outp.tile([P, 512], F32, name="o")
-                outs[(h, r)] = t
-                if (c, r) == ORDER[0]:
-                    vts(bqs[(h, r)][:, 0:256], bb[:, c0:c1], nfb[:, r : r + 1], None, ALU.mult)
-                    nc.scalar.activation(out=bqs[(h, r)][:, 256:512], in_=bb[:, 768:1024], func=ACT.Copy, scale=nfb[:, r : r + 1])
-                else:
-                    nc.scalar.activation(out=bqs[(h, r)][:], in_=bb[:, 512 * h : 512 * (h + 1)], func=ACT.Copy, scale=nfb[:, r : r + 1])
-            lo = c0 - 512 * h
-            hi = c1 - 512 * h
-            vstt(outs[(h, r)][:, lo:hi], mx[(c, r)], fa[:, r : r + 1], bqs[(h, r)][:, lo:hi], ALU.mult, ALU.subtract)
-            if c != 1:
-                nc.sync.dma_start(out=out[P * r : P * (r + 1), 512 * h : 512 * (h + 1)], in_=outs[(h, r)][:])
+            bq = outp.tile([P, 512], F32, name="bq")
+            o = outp.tile([P, 512], F32, name="o")
+            nc.scalar.activation(out=bq[:], in_=bb[:, 512 * c : 512 * (c + 1)], func=ACT.Copy, scale=nfb[:, r : r + 1])
+            vstt(o[:], mx[(c, r)][:], fa[:, r : r + 1], bq[:], ALU.mult, ALU.subtract)
+            nc.sync.dma_start(out=out[P * r : P * (r + 1), 512 * c : 512 * (c + 1)], in_=o[:])

@@ -62,7 +62,6 @@ def tile_directnodecomphyperbolicforecaster_pa_kernel(tc, v_init, W_vel_bytes, W
         ones = keep.tile([P, P], F32, name="ones")
         pb = keep.tile([P, 1], F32, name="pb")
         half = keep.tile([P, 5], F32, name="half")
-        nhalf = keep.tile([P, 5], F32, name="nhalf")
         sx = keep.tile([P, RT + 1], F32, name="sx")
         smp = keep.tile([P, 2, RT], F32, name="smp")
         dp = keep.tile([P, 2, RT], F32, name="dp")
@@ -175,25 +174,20 @@ def tile_directnodecomphyperbolicforecaster_pa_kernel(tc, v_init, W_vel_bytes, W
 
         nc.scalar.dma_start(out=s8[:].rearrange("p (g t) -> p g t", t=4), in_=W_vel_scale.rearrange("o (g p t) -> p (o g) t", p=P, t=4))
         nc.scalar.dma_start(out=b8[:], in_=b_vel.rearrange("(p c) -> p c", c=8))
-        load_w(0)
-        load_w(1)
+        for j in range(4):
+            load_w(j)
         load_x(0)
-        load_w(2)
-        load_w(3)
         load_x(1)
-        load_w(4)
-        load_x(2)
-        load_w(5)
-        load_x(3)
-        load_w(6)
-        load_w(7)
+        for j in range(4, WT):
+            load_w(j)
+            if j < 6:
+                load_x(j - 2)
         nc.sync.dma_start(out=bb[:], in_=b_vel.partition_broadcast(P))
 
         nc.vector.memset(one[:], 1.0)
         make_identity(nc, ident[:])
         nc.vector.memset(ones[:], 1.0)
         nc.vector.memset(half[:], 0.5)
-        nc.vector.memset(nhalf[:], -0.5)
         nc.scalar.activation(out=warm[:], in_=one[:], func=ACT.Ln)
 
         jb = small("jb", 8)
@@ -202,7 +196,9 @@ def tile_directnodecomphyperbolicforecaster_pa_kernel(tc, v_init, W_vel_bytes, W
         for c0 in (0, 512):
             for j in (0, 1):
                 cast(nc.vector, j, c0, c0 + 512)
-        for j in range(2, WT):
+        for j in (2, 3):
+            nc.scalar.copy(out=wb[j][:], in_=wby[j][:].bitcast(FP8))
+        for j in range(4, WT):
             cast(nc.gpsimd, j, 0, K)
         w_turn(0, 0)
         w_turn(0, 1)
@@ -213,16 +209,14 @@ def tile_directnodecomphyperbolicforecaster_pa_kernel(tc, v_init, W_vel_bytes, W
         w_turn(1, 0)
         w_turn(1, 1)
         x_turn(2)
-        xnorm(0)
         nc.scalar.copy(out=sx[:, RT : RT + 1], in_=bsq[:])
         x_copy(0)
         x_copy(1)
         x_turn(3)
-        xnorm(1)
         x_copy(2)
         x_copy(3)
-        xnorm(2)
-        xnorm(3)
+        for i in range(RT):
+            xnorm(i)
         w_exit(0, 0)
         w_exit(0, 1)
         w_turn(2, 0)
@@ -239,96 +233,92 @@ def tile_directnodecomphyperbolicforecaster_pa_kernel(tc, v_init, W_vel_bytes, W
         quant_w(1)
         for r in range(RT):
             mult(1, r)
-        n9 = small("n9", 9)
-        nc.gpsimd.tensor_scalar(out=n9[:, 0:5], in0=sx[:], scalar1=EPS, scalar2=None, op0=ALU.max)
-        nc.gpsimd.tensor_scalar(out=n9[:, 5:9], in0=sx[:, 0:RT], scalar1=EPS, scalar2=CMAX * CMAX, op0=ALU.max, op1=ALU.min)
-        row = small("row", 28)
-        nc.gpsimd.tensor_tensor(out=row[:, 20:25], in0=n9[:, 4:9], in1=half[:], op=ALU.pow)
-        ir = small("ir", 5)
-        nc.gpsimd.tensor_tensor(out=ir[:], in0=n9[:, 0:5], in1=nhalf[:], op=ALU.pow)
-        rb = row[:, 20:21]
-        cx = row[:, 21:25]
+        n5 = small("n5", 5)
+        nc.gpsimd.tensor_scalar(out=n5[:], in0=sx[:], scalar1=EPS, scalar2=None, op0=ALU.max)
+        rt = small("rt", 5)
+        nc.gpsimd.tensor_tensor(out=rt[:], in0=n5[:], in1=half[:], op=ALU.pow)
+        cx = small("cx")
+        nc.gpsimd.tensor_scalar(out=cx[:], in0=rt[:, 0:4], scalar1=CMAX, scalar2=None, op0=ALU.min)
         w_exit(2, 1)
         for r in range(RT):
             square(0, r)
         w_exit(3, 0)
         quant_w(2)
+        ir = small("ir", 5)
+        nc.vector.reciprocal(out=ir[:], in_=rt[:])
         w_exit(3, 1)
         for r in range(RT):
             mult(2, r)
-        dot(0, 0)
         quant_w(3)
         for r in range(RT):
             mult(3, r)
 
         lnp = small("lnp")
-        nc.scalar.activation(out=lnp[:], in_=cx, func=ACT.Ln, bias=1.0)
+        nc.scalar.activation(out=lnp[:], in_=cx[:], func=ACT.Ln, bias=1.0)
         lnq = small("lnq")
-        nc.scalar.activation(out=lnq[:], in_=cx, func=ACT.Ln, scale=-1.0, bias=1.0)
-        for r in range(1, RT):
-            dot(0, r)
-        a01 = small("a01")
-        nc.gpsimd.tensor_scalar(out=a01[:], in0=smp[:, 0, :], scalar1=EPS, scalar2=None, op0=ALU.max)
+        nc.scalar.activation(out=lnq[:], in_=cx[:], func=ACT.Ln, scale=-1.0, bias=1.0)
         at2 = small("at2")
         nc.gpsimd.tensor_tensor(out=at2[:], in0=lnp[:], in1=lnq[:], op=ALU.subtract)
         kp = small("kp")
         nc.gpsimd.tensor_tensor(out=kp[:], in0=at2[:], in1=ir[:, 0:4], op=ALU.mult)
-        ib = ir[:, 4:5]
+        tb = small("tb", 1)
+        nc.scalar.activation(out=tb[:], in_=rt[:, 4:5], func=ACT.Tanh)
+        bk = small("bk", 2)
+        nc.scalar.activation(out=bk[:, 0:1], in_=tb[:], func=ACT.Copy, scale=ir[:, 4:5])
+        q2 = small("q2", 1)
+        nc.scalar.activation(out=q2[:], in_=tb[:], func=ACT.Square)
+        nc.scalar.activation(out=bk[:, 1:2], in_=q2[:], func=ACT.Copy, scale=KF, bias=-KF)
+        kap = small("kap")
+        nc.scalar.activation(out=kap[:], in_=kp[:], func=ACT.Copy, scale=0.5)
+        beta = bk[:, 0:1]
+        s0 = small("s0")
+        nc.gpsimd.tensor_scalar(out=s0[:], in0=smp[:, 0, :], scalar1=EPS, scalar2=None, op0=ALU.max)
 
         for r in range(RT):
             square(1, r)
-        lnk = small("lnk")
-        nc.scalar.activation(out=lnk[:], in_=kp[:], func=ACT.Ln, scale=0.5)
-        lm = small("lm")
+        ss = small("ss")
+        nc.gpsimd.tensor_tensor(out=ss[:], in0=s0[:], in1=smp[:, 1, :], op=ALU.add)
+        m = small("m")
+        nc.gpsimd.tensor_tensor(out=m[:], in0=ss[:], in1=half[:, 0:4], op=ALU.pow)
+        row = small("row", 12)
         for r in range(RT):
-            nc.scalar.activation(out=lm[:, r : r + 1], in_=smp[:, 1, r : r + 1], func=ACT.Ln, bias=a01[:, r : r + 1])
-        dot(1, 0)
-        dot(1, 1)
-        dot(1, 2)
-        lzz = small("lzz", 8)
-        vts(lzz[:, 0:4], lm[:], -0.5, None, ALU.mult)
-        vstt(lzz[:, 4:8], lm[:], 0.5, lnk[:], ALU.mult, ALU.add)
-        dot(1, 3)
-        nc.scalar.activation(out=row[:, 4:28].rearrange("p (a c) -> p a c", a=2)[:, :, 0:4], in_=lzz[:].rearrange("p (a c) -> p a c", a=2), func=ACT.Exp)
-        nc.scalar.activation(out=row[:, 8:13], in_=row[:, 16:21], func=ACT.Tanh)
-        tb = row[:, 12:13]
-        beta = small("beta", 1)
-        nc.scalar.activation(out=beta[:], in_=tb, func=ACT.Copy, scale=ib)
-        q2 = small("q2", 1)
-        nc.scalar.activation(out=q2[:], in_=tb, func=ACT.Square)
-        kq = small("kq", 1)
-        nc.scalar.activation(out=kq[:], in_=q2[:], func=ACT.Copy, scale=KF, bias=-KF)
+            nc.scalar.activation(out=row[:, 8 + r : 9 + r], in_=m[:, r : r + 1], func=ACT.Tanh, scale=kap[:, r : r + 1])
+        for c in range(2):
+            for r in range(RT):
+                dot(c, r)
         db = small("db")
-        nc.vector.tensor_reduce(out=db[:], in_=dp[:].rearrange("p c r -> p r c"), axis=mybir.AxisListType.X, op=ALU.add)
+        vtt(db[:], dp[:, 0, :], dp[:, 1, :], ALU.add)
+        nc.vector.reciprocal(out=row[:, 4:8], in_=m[:])
         vstt(row[:, 0:4], row[:, 4:8], 2.0, db[:], ALU.mult, ALU.mult)
 
         l1 = keep.tile([P, 3, RT], F32, name="l1")
-        vtt(l1[:], row[:, 8:12].unsqueeze(1).to_broadcast([P, 3, RT]), row[:, 0:12].rearrange("p (a r) -> p a r", a=3), ALU.mult)
+        vtt(l1[:], row[:, 8:12].unsqueeze(1).to_broadcast([P, 3, RT]), row[:].rearrange("p (a r) -> p a r", a=3), ALU.mult)
         alpha = l1[:, 1, :]
         t2 = l1[:, 2, :]
-        u3 = keep.tile([P, 3, RT], F32, name="u3")
+        u = keep.tile([P, 4, RT], F32, name="u")
         pe1 = small("pe1")
-        vts(pe1[:], l1[:, 0, :], beta[:], 1.0, ALU.mult, ALU.add)
-        vts(u3[:, 1, :], t2, -1.0, beta[:], ALU.add, ALU.mult)
-        omq = small("omq")
-        vts(omq[:], t2, -1.0, kq[:], ALU.add, ALU.mult)
-        den0 = small("den0")
-        vstt(den0[:], t2, q2[:], pe1[:], ALU.mult, ALU.add)
-        vstt(u3[:, 2, :], pe1[:], q2[:], alpha, ALU.add, ALU.mult)
-        vstt(u3[:, 0, :], den0[:], 1.5 - KF, omq[:], ALU.mult, ALU.add)
+        vts(pe1[:], l1[:, 0, :], beta, 1.0, ALU.mult, ALU.add)
+        vstt(u[:, 1:4:2, :], l1[:, 2:3, :].to_broadcast([P, 2, RT]), -1.0, bk[:].unsqueeze(2).to_broadcast([P, 2, RT]), ALU.add, ALU.mult)
+        den = small("den")
+        vstt(den[:], t2, q2[:], pe1[:], ALU.mult, ALU.add)
+        vstt(u[:, 2, :], pe1[:], q2[:], alpha, ALU.add, ALU.mult)
         rr = small("rr")
-        nc.vector.reciprocal(out=rr[:], in_=den0[:])
+        nc.vector.reciprocal(out=rr[:], in_=den[:])
+        vstt(u[:, 0, :], den[:], 1.5 - KF, u[:, 3, :], ALU.mult, ALU.add)
         v3 = keep.tile([P, 3, RT], F32, name="v3")
-        vstt(v3[:], rr[:].unsqueeze(1).to_broadcast([P, 3, RT]), BIG, u3[:], ALU.min, ALU.mult)
+        vstt(v3[:], rr[:].unsqueeze(1).to_broadcast([P, 3, RT]), BIG, u[:, 0:3, :], ALU.min, ALU.mult)
         ff = keep.tile([P, 2, RT], F32, name="ff")
         vstt(ff[:], v3[:, 0:1, :].to_broadcast([P, 2, RT]), 1.0, v3[:, 1:3, :], ALU.min, ALU.mult)
         nfb = ff[:, 0, :]
         fa = ff[:, 1, :]
 
-        ORDER = [(c, r) for r in range(RT) for c in range(2)]
-        for c, r in ORDER:
-            bq = outp.tile([P, 512], F32, name="bq")
-            o = outp.tile([P, 512], F32, name="o")
-            nc.scalar.activation(out=bq[:], in_=bb[:, 512 * c : 512 * (c + 1)], func=ACT.Copy, scale=nfb[:, r : r + 1])
-            vstt(o[:], mx[(c, r)][:], fa[:, r : r + 1], bq[:], ALU.mult, ALU.subtract)
-            nc.sync.dma_start(out=out[P * r : P * (r + 1), 512 * c : 512 * (c + 1)], in_=o[:])
+        for r in range(RT):
+            for c in range(2):
+                bq = outp.tile([P, 512], F32, name="bq")
+                o = outp.tile([P, 512], F32, name="o")
+                if (c, r) == (0, 0):
+                    vts(bq[:], bb[:, 512 * c : 512 * (c + 1)], nfb[:, r : r + 1], None, ALU.mult)
+                else:
+                    nc.scalar.activation(out=bq[:], in_=bb[:, 512 * c : 512 * (c + 1)], func=ACT.Copy, scale=nfb[:, r : r + 1])
+                vstt(o[:], mx[(c, r)][:], fa[:, r : r + 1], bq[:], ALU.mult, ALU.subtract)
+                nc.sync.dma_start(out=out[P * r : P * (r + 1), 512 * c : 512 * (c + 1)], in_=o[:])

@@ -63,7 +63,7 @@ def tile_directnodecomphyperbolicforecaster_pa_kernel(tc, v_init, W_vel_bytes, W
         pb = keep.tile([P, 1], F32, name="pb")
         half = keep.tile([P, 5], F32, name="half")
         sx = keep.tile([P, RT + 1], F32, name="sx")
-        smp = keep.tile([P, 2, RT], F32, name="smp")
+        smp = keep.tile([P, 4, RT], F32, name="smp")
         dp = keep.tile([P, 2, RT], F32, name="dp")
 
         def small(name, w=4):
@@ -88,19 +88,24 @@ def tile_directnodecomphyperbolicforecaster_pa_kernel(tc, v_init, W_vel_bytes, W
         def cast(engine, j, c0, c1):
             engine.tensor_copy(out=wb[j][:, c0:c1], in_=wby[j][:, c0:c1].bitcast(FP8))
 
-        def w_turn(q, g):
-            t = bank(4 + (2 * q + g) % 4, [P, 2, 2, P], "tw%d_%d" % (q, g))
-            for jj in range(2):
-                words = wb[2 * q + jj][:].bitcast(F32)
-                for u in range(2):
-                    nc.tensor.transpose(t[:, u, jj, :], words[:, 256 * g + u : 256 * (g + 1) : 2], ident[:])
-            banks[("w", q, g)] = t
+        w_banks = [4 + i % 4 for i in range(9)]
 
-        def w_exit(q, g):
+        def w_turn(q, g, tiles=(0, 1)):
+            w = len(tiles) * P
+            t = bank(w_banks.pop(0), [P, 2, w], "tw%d_%d_%d" % (q, g, tiles[0]))
+            for i, j in enumerate(tiles):
+                words = wb[2 * q + j][:].bitcast(F32)
+                for u in range(2):
+                    nc.tensor.transpose(t[:, u, P * i : P * (i + 1)], words[:, 256 * g + u : 256 * (g + 1) : 2], ident[:])
+            banks[("w", q, g, tiles)] = t
+
+        def w_exit(q, g, tiles=(0, 1)):
+            n0 = P * tiles[0]
+            w = len(tiles) * P
             nc.vector.tensor_tensor(
-                out=wg[:, q, g, :, :].rearrange("p n (u e) -> p n u e", e=2),
-                in0=banks[("w", q, g)][:].rearrange("p u j n -> p u (j n)").bitcast(BF16).rearrange("p u (n e) -> p n u e", e=2),
-                in1=s8[:, 4 * g : 4 * g + 4].rearrange("p (u e) -> p u e", e=2).unsqueeze(1).to_broadcast([P, 256, 2, 2]),
+                out=wg[:, q, g, n0 : n0 + w, :].rearrange("p n (u e) -> p n u e", e=2),
+                in0=banks[("w", q, g, tiles)][:].bitcast(BF16).rearrange("p u (n e) -> p n u e", e=2),
+                in1=s8[:, 4 * g : 4 * g + 4].rearrange("p (u e) -> p u e", e=2).unsqueeze(1).to_broadcast([P, w, 2, 2]),
                 op=ALU.mult,
             )
 
@@ -133,7 +138,7 @@ def tile_directnodecomphyperbolicforecaster_pa_kernel(tc, v_init, W_vel_bytes, W
         def mult(q, r):
             c = q // 2
             if q % 2 == 0:
-                mx[(c, r)] = bank(4 * c + r, [P, 512], "mx%d_%d" % (c, r))
+                mx[(c, r)] = bank(r if c == 0 else 4 + (r + 1) % 4, [P, 512], "mx%d_%d" % (c, r))
             for g in range(G):
                 nc.tensor.matmul_mx(
                     out=mx[(c, r)][:, 256 * (q % 2) : 256 * (q % 2 + 1)],
@@ -149,9 +154,10 @@ def tile_directnodecomphyperbolicforecaster_pa_kernel(tc, v_init, W_vel_bytes, W
             junk = work.tile([P, K], BF16, name="junkh")
             nc.scalar.activation(out=junk[:], in_=xin[i][:], func=ACT.Square, accum_out=sx[:, i : i + 1])
 
-        def square(c, r):
-            js = work.tile([P, 512], BF16, name="junks")
-            nc.scalar.activation(out=js[:], in_=mx[(c, r)][:], func=ACT.Square, accum_out=smp[:, c, r : r + 1])
+        def square(q, r):
+            js = work.tile([P, 256], BF16, name="junks")
+            src = mx[(q // 2, r)][:, 256 * (q % 2) : 256 * (q % 2 + 1)]
+            nc.scalar.activation(out=js[:], in_=src, func=ACT.Square, accum_out=smp[:, q, r : r + 1])
 
         def dot(c, r):
             jv = work.tile([P, 512], F32, name="junkv")
@@ -174,14 +180,14 @@ def tile_directnodecomphyperbolicforecaster_pa_kernel(tc, v_init, W_vel_bytes, W
 
         nc.scalar.dma_start(out=s8[:].rearrange("p (g t) -> p g t", t=4), in_=W_vel_scale.rearrange("o (g p t) -> p (o g) t", p=P, t=4))
         nc.scalar.dma_start(out=b8[:], in_=b_vel.rearrange("(p c) -> p c", c=8))
-        for j in range(4):
+        for j in range(5):
             load_w(j)
         load_x(0)
         load_x(1)
-        for j in range(4, WT):
+        for j in range(5, WT):
             load_w(j)
-            if j < 6:
-                load_x(j - 2)
+            if j < 7:
+                load_x(j - 3)
         nc.sync.dma_start(out=bb[:], in_=b_vel.partition_broadcast(P))
 
         nc.vector.memset(one[:], 1.0)
@@ -196,40 +202,46 @@ def tile_directnodecomphyperbolicforecaster_pa_kernel(tc, v_init, W_vel_bytes, W
         for c0 in (0, 512):
             for j in (0, 1):
                 cast(nc.vector, j, c0, c0 + 512)
-        for j in (2, 3):
-            nc.scalar.copy(out=wb[j][:], in_=wby[j][:].bitcast(FP8))
+        for c0 in (0, 512):
+            for j in (2, 3):
+                nc.scalar.copy(out=wb[j][:, c0 : c0 + 512], in_=wby[j][:, c0 : c0 + 512].bitcast(FP8))
         for j in range(4, WT):
             cast(nc.gpsimd, j, 0, K)
-        w_turn(0, 0)
+        w_turn(0, 0, (0,))
+        w_turn(0, 0, (1,))
         w_turn(0, 1)
         bsq = bank(3, [P, 1], "bsq")
         nc.tensor.matmul(out=bsq[:], lhsT=ones[:], rhs=pb[:], start=True, stop=True)
+        w_turn(1, 0)
         x_turn(0)
         x_turn(1)
-        w_turn(1, 0)
+        w_exit(0, 0, (0,))
         w_turn(1, 1)
         x_turn(2)
+        xnorm(0)
         nc.scalar.copy(out=sx[:, RT : RT + 1], in_=bsq[:])
         x_copy(0)
         x_copy(1)
         x_turn(3)
         x_copy(2)
         x_copy(3)
-        for i in range(RT):
+        for i in range(1, RT):
             xnorm(i)
-        w_exit(0, 0)
-        w_exit(0, 1)
+        w_exit(0, 0, (1,))
         w_turn(2, 0)
+        w_exit(0, 1)
         w_turn(2, 1)
         w_exit(1, 0)
-        w_exit(1, 1)
         w_turn(3, 0)
+        w_exit(1, 1)
         w_turn(3, 1)
-        quant_x()
         quant_w(0)
+        quant_x()
         w_exit(2, 0)
         for r in range(RT):
             mult(0, r)
+        for r in range(RT):
+            square(0, r)
         quant_w(1)
         for r in range(RT):
             mult(1, r)
@@ -241,7 +253,7 @@ def tile_directnodecomphyperbolicforecaster_pa_kernel(tc, v_init, W_vel_bytes, W
         nc.gpsimd.tensor_scalar(out=cx[:], in0=rt[:, 0:4], scalar1=CMAX, scalar2=None, op0=ALU.min)
         w_exit(2, 1)
         for r in range(RT):
-            square(0, r)
+            square(1, r)
         w_exit(3, 0)
         quant_w(2)
         ir = small("ir", 5)
@@ -250,8 +262,6 @@ def tile_directnodecomphyperbolicforecaster_pa_kernel(tc, v_init, W_vel_bytes, W
         for r in range(RT):
             mult(2, r)
         quant_w(3)
-        for r in range(RT):
-            mult(3, r)
 
         lnp = small("lnp")
         nc.scalar.activation(out=lnp[:], in_=cx[:], func=ACT.Ln, bias=1.0)
@@ -271,54 +281,130 @@ def tile_directnodecomphyperbolicforecaster_pa_kernel(tc, v_init, W_vel_bytes, W
         kap = small("kap")
         nc.scalar.activation(out=kap[:], in_=kp[:], func=ACT.Copy, scale=0.5)
         beta = bk[:, 0:1]
+        for r in range(RT):
+            square(2, r)
+        for r in range(RT):
+            mult(3, r)
         s0 = small("s0")
         nc.gpsimd.tensor_scalar(out=s0[:], in0=smp[:, 0, :], scalar1=EPS, scalar2=None, op0=ALU.max)
+        s1 = small("s1")
+        nc.gpsimd.tensor_tensor(out=s1[:], in0=s0[:], in1=smp[:, 1, :], op=ALU.add)
+        s2 = small("s2")
+        nc.gpsimd.tensor_tensor(out=s2[:], in0=s1[:], in1=smp[:, 2, :], op=ALU.add)
 
         for r in range(RT):
-            square(1, r)
-        ss = small("ss")
-        nc.gpsimd.tensor_tensor(out=ss[:], in0=s0[:], in1=smp[:, 1, :], op=ALU.add)
-        m = small("m")
-        nc.gpsimd.tensor_tensor(out=m[:], in0=ss[:], in1=half[:, 0:4], op=ALU.pow)
-        row = small("row", 12)
-        for r in range(RT):
-            nc.scalar.activation(out=row[:, 8 + r : 9 + r], in_=m[:, r : r + 1], func=ACT.Tanh, scale=kap[:, r : r + 1])
-        for c in range(2):
-            for r in range(RT):
-                dot(c, r)
-        db = small("db")
-        vtt(db[:], dp[:, 0, :], dp[:, 1, :], ALU.add)
-        nc.vector.reciprocal(out=row[:, 4:8], in_=m[:])
-        vstt(row[:, 0:4], row[:, 4:8], 2.0, db[:], ALU.mult, ALU.mult)
+            square(3, r)
+        st = []
+        for h in range(2):
+            d = {}
+            for name, w in (("ss", 2), ("m", 2), ("db", 2), ("row", 6), ("l1", 6), ("pe1", 2), ("u", 8), ("den", 2), ("rr", 2), ("v3", 6), ("ff", 4)):
+                d[name] = small("%s_%d" % (name, h), w)
+            st.append(d)
 
-        l1 = keep.tile([P, 3, RT], F32, name="l1")
-        vtt(l1[:], row[:, 8:12].unsqueeze(1).to_broadcast([P, 3, RT]), row[:].rearrange("p (a r) -> p a r", a=3), ALU.mult)
-        alpha = l1[:, 1, :]
-        t2 = l1[:, 2, :]
-        u = keep.tile([P, 4, RT], F32, name="u")
-        pe1 = small("pe1")
-        vts(pe1[:], l1[:, 0, :], beta, 1.0, ALU.mult, ALU.add)
-        vstt(u[:, 1:4:2, :], l1[:, 2:3, :].to_broadcast([P, 2, RT]), -1.0, bk[:].unsqueeze(2).to_broadcast([P, 2, RT]), ALU.add, ALU.mult)
-        den = small("den")
-        vstt(den[:], t2, q2[:], pe1[:], ALU.mult, ALU.add)
-        vstt(u[:, 2, :], pe1[:], q2[:], alpha, ALU.add, ALU.mult)
-        rr = small("rr")
-        nc.vector.reciprocal(out=rr[:], in_=den[:])
-        vstt(u[:, 0, :], den[:], 1.5 - KF, u[:, 3, :], ALU.mult, ALU.add)
-        v3 = keep.tile([P, 3, RT], F32, name="v3")
-        vstt(v3[:], rr[:].unsqueeze(1).to_broadcast([P, 3, RT]), BIG, u[:, 0:3, :], ALU.min, ALU.mult)
-        ff = keep.tile([P, 2, RT], F32, name="ff")
-        vstt(ff[:], v3[:, 0:1, :].to_broadcast([P, 2, RT]), 1.0, v3[:, 1:3, :], ALU.min, ALU.mult)
-        nfb = ff[:, 0, :]
-        fa = ff[:, 1, :]
+        def by_rows(t):
+            return t[:].rearrange("p (a r) -> p a r", r=2)
 
-        for r in range(RT):
+        def c_m(h):
+            d = st[h]
+            nc.gpsimd.tensor_tensor(out=d["ss"][:], in0=s2[:, 2 * h : 2 * h + 2], in1=smp[:, 3, 2 * h : 2 * h + 2], op=ALU.add)
+            nc.gpsimd.tensor_tensor(out=d["m"][:], in0=d["ss"][:], in1=half[:, 0:2], op=ALU.pow)
+            for k in range(2):
+                nc.scalar.activation(out=d["row"][:, 4 + k : 5 + k], in_=d["m"][:, k : k + 1], func=ACT.Tanh, scale=kap[:, 2 * h + k : 2 * h + k + 1])
+
+        def c_r(h):
+            d = st[h]
+            nc.vector.reciprocal(out=d["row"][:, 2:4], in_=d["m"][:])
+
+        def c_d(h):
+            vtt(st[h]["db"][:], dp[:, 0, 2 * h : 2 * h + 2], dp[:, 1, 2 * h : 2 * h + 2], ALU.add)
+
+        def c_e(h):
+            d = st[h]
+            vstt(d["row"][:, 0:2], d["row"][:, 2:4], 2.0, d["db"][:], ALU.mult, ALU.mult)
+
+        def c_l(h):
+            d = st[h]
+            vtt(by_rows(d["l1"]), d["row"][:, 4:6].unsqueeze(1).to_broadcast([P, 3, 2]), by_rows(d["row"]), ALU.mult)
+
+        def c_u(h):
+            d = st[h]
+            vts(d["pe1"][:], d["l1"][:, 0:2], beta, 1.0, ALU.mult, ALU.add)
+            vstt(
+                by_rows(d["u"])[:, 1:4:2, :], d["l1"][:, 4:6].unsqueeze(1).to_broadcast([P, 2, 2]), -1.0,
+                bk[:].unsqueeze(2).to_broadcast([P, 2, 2]), ALU.add, ALU.mult,
+            )
+
+        def c_den(h):
+            d = st[h]
+            vstt(d["den"][:], d["l1"][:, 4:6], q2[:], d["pe1"][:], ALU.mult, ALU.add)
+            vstt(d["u"][:, 4:6], d["pe1"][:], q2[:], d["l1"][:, 2:4], ALU.add, ALU.mult)
+
+        def c_g(h):
+            d = st[h]
+            nc.vector.reciprocal(out=d["rr"][:], in_=d["den"][:])
+            vstt(d["u"][:, 0:2], d["den"][:], 1.5 - KF, d["u"][:, 6:8], ALU.mult, ALU.add)
+
+        def c_v(h):
+            d = st[h]
+            vstt(by_rows(d["v3"]), d["rr"][:].unsqueeze(1).to_broadcast([P, 3, 2]), BIG, by_rows(d["u"])[:, 0:3, :], ALU.min, ALU.mult)
+
+        def c_f(h):
+            d = st[h]
+            vstt(by_rows(d["ff"]), by_rows(d["v3"])[:, 0:1, :].to_broadcast([P, 2, 2]), 1.0, by_rows(d["v3"])[:, 1:3, :], ALU.min, ALU.mult)
+
+        bqs = {}
+
+        def prod_b(c, r, on_vector=False):
+            nfb = st[r // 2]["ff"][:, r % 2 : r % 2 + 1]
+            bq = outp.tile([P, 512], F32, name="bq")
+            if on_vector:
+                vts(bq[:], bb[:, 512 * c : 512 * (c + 1)], nfb, None, ALU.mult)
+            else:
+                nc.scalar.activation(out=bq[:], in_=bb[:, 512 * c : 512 * (c + 1)], func=ACT.Copy, scale=nfb)
+            bqs[(c, r)] = bq
+
+        def final(c, r):
+            fa = st[r // 2]["ff"][:, 2 + r % 2 : 3 + r % 2]
+            o = outp.tile([P, 512], F32, name="o")
+            vstt(o[:], mx[(c, r)][:], fa, bqs[(c, r)][:], ALU.mult, ALU.subtract)
+            nc.sync.dma_start(out=out[P * r : P * (r + 1), 512 * c : 512 * (c + 1)], in_=o[:])
+
+        c_m(0)
+        c_m(1)
+        dot(0, 0)
+        dot(0, 1)
+        dot(0, 2)
+        dot(1, 0)
+        dot(1, 1)
+        dot(0, 3)
+        c_r(0)
+        c_d(0)
+        c_e(0)
+        c_l(0)
+        dot(1, 2)
+        c_u(0)
+        dot(1, 3)
+        c_den(0)
+        c_r(1)
+        c_d(1)
+        c_g(0)
+        c_e(1)
+        c_v(0)
+        c_l(1)
+        c_f(0)
+        c_u(1)
+        prod_b(0, 0, on_vector=True)
+        for c, r in ((1, 0), (0, 1), (1, 1)):
+            prod_b(c, r)
+        c_den(1)
+        final(0, 0)
+        c_g(1)
+        c_v(1)
+        final(1, 0)
+        c_f(1)
+        final(0, 1)
+        final(1, 1)
+        for r in (2, 3):
             for c in range(2):
-                bq = outp.tile([P, 512], F32, name="bq")
-                o = outp.tile([P, 512], F32, name="o")
-                if (c, r) == (0, 0):
-                    vts(bq[:], bb[:, 512 * c : 512 * (c + 1)], nfb[:, r : r + 1], None, ALU.mult)
-                else:
-                    nc.scalar.activation(out=bq[:], in_=bb[:, 512 * c : 512 * (c + 1)], func=ACT.Copy, scale=nfb[:, r : r + 1])
-                vstt(o[:], mx[(c, r)][:], fa[:, r : r + 1], bq[:], ALU.mult, ALU.subtract)
-                nc.sync.dma_start(out=out[P * r : P * (r + 1), 512 * c : 512 * (c + 1)], in_=o[:])
+                prod_b(c, r)
+                final(c, r)

@@ -207,6 +207,11 @@ def tile_directnodecomphyperbolicforecaster_pa_kernel(tc, v_init, W_vel_bytes, W
                 nc.scalar.copy(out=wb[j][:, c0 : c0 + 512], in_=wby[j][:, c0 : c0 + 512].bitcast(FP8))
         for j in range(4, WT):
             cast(nc.gpsimd, j, 0, K)
+        def keep_warm(i, count):
+            t = bank(i, [P, 512], "warm%d_%d" % (i, count))
+            for k in range(count):
+                nc.tensor.matmul(out=t[:], lhsT=xin[0][:, 0:P], rhs=xin[0][:, 0:512], start=True, stop=True)
+
         w_turn(0, 0, (0,))
         w_turn(0, 0, (1,))
         w_turn(0, 1)
@@ -231,10 +236,12 @@ def tile_directnodecomphyperbolicforecaster_pa_kernel(tc, v_init, W_vel_bytes, W
         w_turn(2, 0)
         w_exit(0, 1)
         w_turn(2, 1)
+        keep_warm(0, 2)
         w_exit(1, 0)
         w_turn(3, 0)
         w_exit(1, 1)
         w_turn(3, 1)
+        keep_warm(1, 2)
         quant_w(0)
         quant_x()
         w_exit(2, 0)
@@ -245,6 +252,7 @@ def tile_directnodecomphyperbolicforecaster_pa_kernel(tc, v_init, W_vel_bytes, W
         quant_w(1)
         for r in range(RT):
             mult(1, r)
+        keep_warm(5, 1)
         n5 = small("n5", 5)
         nc.gpsimd.tensor_scalar(out=n5[:], in0=sx[:], scalar1=EPS, scalar2=None, op0=ALU.max)
         rt = small("rt", 5)
@@ -273,14 +281,8 @@ def tile_directnodecomphyperbolicforecaster_pa_kernel(tc, v_init, W_vel_bytes, W
         nc.gpsimd.tensor_tensor(out=kp[:], in0=at2[:], in1=ir[:, 0:4], op=ALU.mult)
         tb = small("tb", 1)
         nc.scalar.activation(out=tb[:], in_=rt[:, 4:5], func=ACT.Tanh)
-        bk = small("bk", 2)
-        nc.scalar.activation(out=bk[:, 0:1], in_=tb[:], func=ACT.Copy, scale=ir[:, 4:5])
-        q2 = small("q2", 1)
-        nc.scalar.activation(out=q2[:], in_=tb[:], func=ACT.Square)
-        nc.scalar.activation(out=bk[:, 1:2], in_=q2[:], func=ACT.Copy, scale=KF, bias=-KF)
         kap = small("kap")
         nc.scalar.activation(out=kap[:], in_=kp[:], func=ACT.Copy, scale=0.5)
-        beta = bk[:, 0:1]
         for r in range(RT):
             square(2, r)
         for r in range(RT):
@@ -292,12 +294,22 @@ def tile_directnodecomphyperbolicforecaster_pa_kernel(tc, v_init, W_vel_bytes, W
         s2 = small("s2")
         nc.gpsimd.tensor_tensor(out=s2[:], in0=s1[:], in1=smp[:, 2, :], op=ALU.add)
 
+        ss = small("ss")
         for r in range(RT):
             square(3, r)
+            if r % 2 == 1:
+                for i in (r - 1, r):
+                    nc.scalar.activation(out=ss[:, i : i + 1], in_=smp[:, 3, i : i + 1], func=ACT.Identity, bias=s2[:, i : i + 1])
+        bk = small("bk", 2)
+        nc.scalar.activation(out=bk[:, 0:1], in_=tb[:], func=ACT.Copy, scale=ir[:, 4:5])
+        q2 = small("q2", 1)
+        nc.scalar.activation(out=q2[:], in_=tb[:], func=ACT.Square)
+        nc.scalar.activation(out=bk[:, 1:2], in_=q2[:], func=ACT.Copy, scale=KF, bias=-KF)
+        beta = bk[:, 0:1]
         st = []
         for h in range(2):
             d = {}
-            for name, w in (("ss", 2), ("m", 2), ("db", 2), ("row", 6), ("l1", 6), ("pe1", 2), ("u", 8), ("den", 2), ("rr", 2), ("v3", 6), ("ff", 4)):
+            for name, w in (("m", 2), ("db", 2), ("row", 6), ("l1", 6), ("pe1", 2), ("u", 8), ("den", 2), ("rr", 2), ("v3", 6), ("ff", 4)):
                 d[name] = small("%s_%d" % (name, h), w)
             st.append(d)
 
@@ -306,8 +318,7 @@ def tile_directnodecomphyperbolicforecaster_pa_kernel(tc, v_init, W_vel_bytes, W
 
         def c_m(h):
             d = st[h]
-            nc.gpsimd.tensor_tensor(out=d["ss"][:], in0=s2[:, 2 * h : 2 * h + 2], in1=smp[:, 3, 2 * h : 2 * h + 2], op=ALU.add)
-            nc.gpsimd.tensor_tensor(out=d["m"][:], in0=d["ss"][:], in1=half[:, 0:2], op=ALU.pow)
+            nc.gpsimd.tensor_tensor(out=d["m"][:], in0=ss[:, 2 * h : 2 * h + 2], in1=half[:, 0:2], op=ALU.pow)
             for k in range(2):
                 nc.scalar.activation(out=d["row"][:, 4 + k : 5 + k], in_=d["m"][:, k : k + 1], func=ACT.Tanh, scale=kap[:, 2 * h + k : 2 * h + k + 1])
 
@@ -376,27 +387,27 @@ def tile_directnodecomphyperbolicforecaster_pa_kernel(tc, v_init, W_vel_bytes, W
         dot(0, 2)
         dot(1, 0)
         dot(1, 1)
-        dot(0, 3)
         c_r(0)
         c_d(0)
+        dot(0, 3)
         c_e(0)
-        c_l(0)
         dot(1, 2)
-        c_u(0)
-        dot(1, 3)
-        c_den(0)
+        c_l(0)
         c_r(1)
+        dot(1, 3)
+        c_u(0)
         c_d(1)
-        c_g(0)
+        c_den(0)
         c_e(1)
+        c_g(0)
         c_v(0)
         c_l(1)
         c_f(0)
         c_u(1)
+        c_den(1)
         prod_b(0, 0, on_vector=True)
         for c, r in ((1, 0), (0, 1), (1, 1)):
             prod_b(c, r)
-        c_den(1)
         final(0, 0)
         c_g(1)
         c_v(1)

@@ -162,7 +162,7 @@ def tile_directnodecomphyperbolicforecaster_pa_kernel(tc, v_init, W_vel_bytes, W
         def dot(c, r):
             jv = work.tile([P, 512], F32, name="junkv")
             nc.vector.scalar_tensor_tensor(
-                out=jv[:], in0=mx[(c, r)][:], scalar=1.0, in1=bb[:, 512 * c : 512 * (c + 1)],
+                out=jv[:], in0=mx[(c, r)][:], scalar=2.0, in1=bb[:, 512 * c : 512 * (c + 1)],
                 op0=ALU.mult, op1=ALU.mult, accum_out=dp[:, c, r : r + 1],
             )
 
@@ -305,11 +305,15 @@ def tile_directnodecomphyperbolicforecaster_pa_kernel(tc, v_init, W_vel_bytes, W
         q2 = small("q2", 1)
         nc.scalar.activation(out=q2[:], in_=tb[:], func=ACT.Square)
         nc.scalar.activation(out=bk[:, 1:2], in_=q2[:], func=ACT.Copy, scale=KF, bias=-KF)
+        nbk = small("nbk", 2)
+        nc.scalar.activation(out=nbk[:], in_=bk[:], func=ACT.Copy, scale=-1.0)
+        q2p1 = small("q2p1", 1)
+        nc.scalar.activation(out=q2p1[:], in_=q2[:], func=ACT.Copy, bias=1.0)
         beta = bk[:, 0:1]
         st = []
         for h in range(2):
             d = {}
-            for name, w in (("m", 2), ("db", 2), ("row", 6), ("l1", 6), ("pe1", 2), ("u", 8), ("den", 2), ("rr", 2), ("v3", 6), ("ff", 4)):
+            for name, w in (("m", 2), ("db", 2), ("rm", 2), ("th", 2), ("t2", 2), ("c1", 2), ("al", 2), ("y", 2), ("u", 6), ("omq", 2), ("den", 2), ("rr", 2), ("v3", 6), ("ff", 4)):
                 d[name] = small("%s_%d" % (name, h), w)
             st.append(d)
 
@@ -320,44 +324,44 @@ def tile_directnodecomphyperbolicforecaster_pa_kernel(tc, v_init, W_vel_bytes, W
             d = st[h]
             nc.gpsimd.tensor_tensor(out=d["m"][:], in0=ss[:, 2 * h : 2 * h + 2], in1=half[:, 0:2], op=ALU.pow)
             for k in range(2):
-                nc.scalar.activation(out=d["row"][:, 4 + k : 5 + k], in_=d["m"][:, k : k + 1], func=ACT.Tanh, scale=kap[:, 2 * h + k : 2 * h + k + 1])
-
-        def c_r(h):
-            d = st[h]
-            nc.vector.reciprocal(out=d["row"][:, 2:4], in_=d["m"][:])
+                nc.scalar.activation(out=d["th"][:, k : k + 1], in_=d["m"][:, k : k + 1], func=ACT.Tanh, scale=kap[:, 2 * h + k : 2 * h + k + 1])
+            nc.scalar.activation(out=d["t2"][:], in_=d["th"][:], func=ACT.Square)
+            nc.scalar.activation(out=d["c1"][:], in_=d["t2"][:], func=ACT.Identity, scale=q2[:], bias=1.0)
+            for i, t in enumerate((d["u"][:, 2:4], d["omq"][:])):
+                nc.scalar.activation(out=t, in_=d["t2"][:], func=ACT.Identity, scale=bk[:, i : i + 1], bias=nbk[:, i : i + 1])
 
         def c_d(h):
-            vtt(st[h]["db"][:], dp[:, 0, 2 * h : 2 * h + 2], dp[:, 1, 2 * h : 2 * h + 2], ALU.add)
+            if h == 0:
+                vtt(st[h]["db"][:], dp[:, 0, 0:2], dp[:, 1, 0:2], ALU.add)
+                return
+            for k in range(2):
+                r = 2 * h + k
+                nc.scalar.activation(out=st[h]["db"][:, k : k + 1], in_=dp[:, 1, r : r + 1], func=ACT.Identity, bias=dp[:, 0, r : r + 1])
 
-        def c_e(h):
-            d = st[h]
-            vstt(d["row"][:, 0:2], d["row"][:, 2:4], 2.0, d["db"][:], ALU.mult, ALU.mult)
+        def c_r(h):
+            nc.vector.reciprocal(out=st[h]["rm"][:], in_=st[h]["m"][:])
 
-        def c_l(h):
+        def c_a(h):
             d = st[h]
-            vtt(by_rows(d["l1"]), d["row"][:, 4:6].unsqueeze(1).to_broadcast([P, 3, 2]), by_rows(d["row"]), ALU.mult)
+            vtt(d["al"][:], d["th"][:], d["rm"][:], ALU.mult)
 
-        def c_u(h):
+        def c_y(h):
             d = st[h]
-            vts(d["pe1"][:], d["l1"][:, 0:2], beta, 1.0, ALU.mult, ALU.add)
-            vstt(
-                by_rows(d["u"])[:, 1:4:2, :], d["l1"][:, 4:6].unsqueeze(1).to_broadcast([P, 2, 2]), -1.0,
-                bk[:].unsqueeze(2).to_broadcast([P, 2, 2]), ALU.add, ALU.mult,
-            )
+            vstt(d["y"][:], d["al"][:], beta, d["db"][:], ALU.mult, ALU.mult)
 
         def c_den(h):
             d = st[h]
-            vstt(d["den"][:], d["l1"][:, 4:6], q2[:], d["pe1"][:], ALU.mult, ALU.add)
-            vstt(d["u"][:, 4:6], d["pe1"][:], q2[:], d["l1"][:, 2:4], ALU.add, ALU.mult)
+            vtt(d["den"][:], d["y"][:], d["c1"][:], ALU.add)
+            vstt(d["u"][:, 4:6], d["y"][:], q2p1[:], d["al"][:], ALU.add, ALU.mult)
 
         def c_g(h):
             d = st[h]
             nc.vector.reciprocal(out=d["rr"][:], in_=d["den"][:])
-            vstt(d["u"][:, 0:2], d["den"][:], 1.5 - KF, d["u"][:, 6:8], ALU.mult, ALU.add)
+            vstt(d["u"][:, 0:2], d["den"][:], 1.5 - KF, d["omq"][:], ALU.mult, ALU.add)
 
         def c_v(h):
             d = st[h]
-            vstt(by_rows(d["v3"]), d["rr"][:].unsqueeze(1).to_broadcast([P, 3, 2]), BIG, by_rows(d["u"])[:, 0:3, :], ALU.min, ALU.mult)
+            vstt(by_rows(d["v3"]), d["rr"][:].unsqueeze(1).to_broadcast([P, 3, 2]), BIG, by_rows(d["u"]), ALU.min, ALU.mult)
 
         def c_f(h):
             d = st[h]
@@ -381,7 +385,6 @@ def tile_directnodecomphyperbolicforecaster_pa_kernel(tc, v_init, W_vel_bytes, W
             nc.sync.dma_start(out=out[P * r : P * (r + 1), 512 * c : 512 * (c + 1)], in_=o[:])
 
         c_m(0)
-        c_m(1)
         dot(0, 0)
         dot(0, 1)
         dot(0, 2)
@@ -389,27 +392,26 @@ def tile_directnodecomphyperbolicforecaster_pa_kernel(tc, v_init, W_vel_bytes, W
         dot(1, 1)
         c_r(0)
         c_d(0)
+        c_m(1)
         dot(0, 3)
-        c_e(0)
+        c_a(0)
         dot(1, 2)
-        c_l(0)
+        c_y(0)
         c_r(1)
         dot(1, 3)
-        c_u(0)
-        c_d(1)
         c_den(0)
-        c_e(1)
+        c_d(1)
+        c_a(1)
         c_g(0)
         c_v(0)
-        c_l(1)
+        c_y(1)
         c_f(0)
-        c_u(1)
         c_den(1)
         prod_b(0, 0, on_vector=True)
         for c, r in ((1, 0), (0, 1), (1, 1)):
             prod_b(c, r)
-        final(0, 0)
         c_g(1)
+        final(0, 0)
         c_v(1)
         final(1, 0)
         c_f(1)

@@ -227,13 +227,13 @@ def tile_directnodecomphyperbolicforecaster_pa_kernel(tc, v_init, W_vel_bytes, W
         nc.scalar.copy(out=sx[:, RT : RT + 1], in_=bsq[:])
         x_copy(0)
         x_copy(1)
+        w_exit(0, 0, (1,))
+        w_turn(2, 0)
         x_turn(3)
         x_copy(2)
         x_copy(3)
         for i in range(1, RT):
             xnorm(i)
-        w_exit(0, 0, (1,))
-        w_turn(2, 0)
         w_exit(0, 1)
         w_turn(2, 1)
         keep_warm(0, 2)
@@ -242,9 +242,9 @@ def tile_directnodecomphyperbolicforecaster_pa_kernel(tc, v_init, W_vel_bytes, W
         w_exit(1, 1)
         w_turn(3, 1)
         keep_warm(1, 2)
-        quant_w(0)
-        quant_x()
         w_exit(2, 0)
+        quant_x()
+        quant_w(0)
         for r in range(RT):
             mult(0, r)
         for r in range(RT):

@@ -196,15 +196,14 @@ def tile_directnodecomphyperbolicforecaster_pa_kernel(tc, v_init, W_vel_bytes, W
         nc.vector.memset(half[:], 0.5)
         nc.scalar.activation(out=warm[:], in_=one[:], func=ACT.Ln)
 
+        nc.scalar.copy(out=wb[1][:, 512:K], in_=wby[1][:, 512:K].bitcast(FP8))
         jb = small("jb", 8)
         nc.scalar.activation(out=jb[:], in_=b8[:], func=ACT.Square, accum_out=pb[:])
 
-        for c0 in (0, 512):
-            for j in (0, 1):
-                cast(nc.vector, j, c0, c0 + 512)
-        for c0 in (0, 512):
-            for j in (2, 3):
-                nc.scalar.copy(out=wb[j][:, c0 : c0 + 512], in_=wby[j][:, c0 : c0 + 512].bitcast(FP8))
+        for j, c0 in ((0, 0), (1, 0), (0, 512), (3, 512)):
+            cast(nc.vector, j, c0, c0 + 512)
+        for j, c0 in ((2, 0), (3, 0), (2, 512)):
+            nc.scalar.copy(out=wb[j][:, c0 : c0 + 512], in_=wby[j][:, c0 : c0 + 512].bitcast(FP8))
         for j in range(4, WT):
             cast(nc.gpsimd, j, 0, K)
         def keep_warm(i, count):
@@ -231,8 +230,9 @@ def tile_directnodecomphyperbolicforecaster_pa_kernel(tc, v_init, W_vel_bytes, W
         w_turn(2, 0)
         x_turn(3)
         x_copy(2)
+        xnorm(1)
         x_copy(3)
-        for i in range(1, RT):
+        for i in range(2, RT):
             xnorm(i)
         w_exit(0, 1)
         w_turn(2, 1)

from contextlib import ExitStack

import concourse.mybir as mybir
from concourse.masks import make_identity

FLOPS = 2 * 512 * 1024 * 1024

F32 = mybir.dt.float32
BF16 = mybir.dt.bfloat16
U32 = mybir.dt.uint32
U8 = mybir.dt.uint8
FP8 = mybir.dt.float8_e4m3fn
FP8X4 = mybir.dt.float8_e4m3fn_x4
ALU = mybir.AluOpType
ACT = mybir.ActivationFunctionType

P = 128
ROWS = 512
K = 1024
N = 1024
RT = ROWS // P
WT = N // P
G = K // 512
EPS = 1e-15
CMAX = 1.0 - 1e-7
MAXN = 1.0 - 1e-5
KF = 0.5 / (MAXN * MAXN)
BIG = 1.0 / EPS


def tile_directnodecomphyperbolicforecaster_pa_kernel(tc, v_init, W_vel_bytes, W_vel_scale, b_vel, out):
    nc = tc.nc
    with ExitStack() as ctx:
        keep = ctx.enter_context(tc.tile_pool(name="keep", bufs=1))
        byt = ctx.enter_context(tc.tile_pool(name="byt", bufs=1))
        work = ctx.enter_context(tc.tile_pool(name="work", bufs=2))
        outp = ctx.enter_context(tc.tile_pool(name="outp", bufs=8))
        psum = ctx.enter_context(tc.psum_pool(name="psum", bufs=1))
        ctx.enter_context(tc.manual_schedule())

        b8 = keep.tile([P, 8], BF16, name="b8")
        bb = keep.tile([P, N], BF16, name="bb")
        wby = []
        for j in range(WT):
            t = byt.tile([P, K], U8, name="wby%d" % j)
            wby.append(t)
        xin = []
        for i in range(RT):
            t = keep.tile([P, K], BF16, name="xin%d" % i)
            xin.append(t)
        xg = keep.tile([P, G, ROWS, 4], BF16, name="xg", align_bytes=64)
        wg = keep.tile([P, 4, G, 256, 4], BF16, name="wg", align_bytes=64)
        xc = keep.tile([P, G, ROWS], U32, name="xc", align_bytes=64)
        xsc = keep.tile([P, G, ROWS], U8, name="xsc", align_bytes=64)
        wc = keep.tile([P, 4, G, 256], U32, name="wc", align_bytes=64)
        wsc = keep.tile([P, 4, G, 256], U8, name="wsc", align_bytes=64)
        xgw = xg[:].bitcast(F32)
        one = keep.tile([P, 1], F32, name="one")
        warm = keep.tile([P, 1], F32, name="warm")
        ident = keep.tile([P, P], F32, name="ident")
        s8 = keep.tile([P, 8], F32, name="s8")
        ones = keep.tile([P, P], F32, name="ones")
        pb = keep.tile([P, 1], F32, name="pb")
        half = keep.tile([P, 5], F32, name="half")
        sx = keep.tile([P, RT + 1], F32, name="sx")
        smp = keep.tile([P, 4, RT], F32, name="smp")
        dp = keep.tile([P, 2, RT], F32, name="dp")

        def small(name, w=4):
            return keep.tile([P, w], F32, name=name)

        def bank(i, shape, name):
            return psum.tile(shape, F32, tag="b%d" % i, name=name)

        def load_x(i):
            nc.sync.dma_start(out=xin[i][:], in_=v_init[P * i : P * (i + 1), :])

        def load_w(j):
            nc.sync.dma_start(out=wby[j][:], in_=W_vel_bytes[P * j : P * (j + 1), :])

        banks = {}

        wb = []
        for j in range(WT):
            t = keep.tile([P, K], BF16, name="wb%d" % j)
            wb.append(t)

        def cast(engine, j, c0, c1):
            engine.tensor_copy(out=wb[j][:, c0:c1], in_=wby[j][:, c0:c1].bitcast(FP8))

        w_banks = [4 + i % 4 for i in range(9)]

        def w_turn(q, g, tiles=(0, 1)):
            w = len(tiles) * P
            t = bank(w_banks.pop(0), [P, 2, w], "tw%d_%d_%d" % (q, g, tiles[0]))
            for i, j in enumerate(tiles):
                words = wb[2 * q + j][:].bitcast(F32)
                for u in range(2):
                    nc.tensor.transpose(t[:, u, P * i : P * (i + 1)], words[:, 256 * g + u : 256 * (g + 1) : 2], ident[:])
            banks[("w", q, g, tiles)] = t

        def w_exit(q, g, tiles=(0, 1)):
            n0 = P * tiles[0]
            w = len(tiles) * P
            nc.vector.tensor_tensor(
                out=wg[:, q, g, n0 : n0 + w, :].rearrange("p n (u e) -> p n u e", e=2),
                in0=banks[("w", q, g, tiles)][:].bitcast(BF16).rearrange("p u (n e) -> p n u e", e=2),
                in1=s8[:, 4 * g : 4 * g + 4].rearrange("p (u e) -> p u e", e=2).unsqueeze(1).to_broadcast([P, w, 2, 2]),
                op=ALU.mult,
            )

        def x_turn(i):
            words = xin[i][:].bitcast(F32)
            t = bank(i, [P, G, 2, P], "tx%d" % i)
            for g in range(G):
                for u in range(2):
                    nc.tensor.transpose(t[:, g, u, :], words[:, 256 * g + u : 256 * (g + 1) : 2], ident[:])
            banks[("x", i)] = t

        def x_copy(i):
            nc.scalar.copy(out=xgw[:, :, P * i : P * (i + 1), :], in_=banks[("x", i)][:].rearrange("p g u n -> p g n u"))

        def quant_x():
            nc.vector.quantize_mx(
                out=xc[:].rearrange("p g n -> p (g n)").bitcast(FP8X4), scales=xsc[:].rearrange("p g n -> p (g n)"),
                in_=xg[:].rearrange("p g n t -> p (g n t)"),
            )

        def quant_w(q):
            nc.vector.quantize_mx(
                out=wc[:, q, :, :].rearrange("p g n -> p (g n)").bitcast(FP8X4),
                scales=wsc[:, q, :, :].rearrange("p g n -> p (g n)"),
                in_=wg[:, q, :, :, :].rearrange("p g n t -> p (g n t)"),
            )

        mx = {}

        def mult(q, r):
            c = q // 2
            if q % 2 == 0:
                mx[(c, r)] = bank(r if c == 0 else 4 + (r + 1) % 4, [P, 512], "mx%d_%d" % (c, r))
            for g in range(G):
                nc.tensor.matmul_mx(
                    out=mx[(c, r)][:, 256 * (q % 2) : 256 * (q % 2 + 1)],
                    lhsT=xc[:, g, P * r : P * (r + 1)].bitcast(FP8X4),
                    lhsT_scale=xsc[:, g, P * r : P * (r + 1)],
                    rhs=wc[:, q, g, :].bitcast(FP8X4),
                    rhs_scale=wsc[:, q, g, :],
                    start=(g == 0),
                    stop=(g == G - 1),
                )

        def xnorm(i):
            junk = work.tile([P, K], BF16, name="junkh")
            nc.scalar.activation(out=junk[:], in_=xin[i][:], func=ACT.Square, accum_out=sx[:, i : i + 1])

        def square(q, r):
            js = work.tile([P, 256], BF16, name="junks")
            src = mx[(q // 2, r)][:, 256 * (q % 2) : 256 * (q % 2 + 1)]
            nc.scalar.activation(out=js[:], in_=src, func=ACT.Square, accum_out=smp[:, q, r : r + 1])

        def dot(c, r):
            jv = work.tile([P, 512], F32, name="junkv")
            nc.vector.scalar_tensor_tensor(
                out=jv[:], in0=mx[(c, r)][:], scalar=2.0, in1=bb[:, 512 * c : 512 * (c + 1)],
                op0=ALU.mult, op1=ALU.mult, accum_out=dp[:, c, r : r + 1],
            )

        def vts(o, i0, s1, s2, op0, op1=None):
            if op1 is None:
                nc.vector.tensor_scalar(out=o, in0=i0, scalar1=s1, scalar2=None, op0=op0)
            else:
                nc.vector.tensor_scalar(out=o, in0=i0, scalar1=s1, scalar2=s2, op0=op0, op1=op1)

        def vtt(o, i0, i1, op):
            nc.vector.tensor_tensor(out=o, in0=i0, in1=i1, op=op)

        def vstt(o, i0, s, i1, op0, op1):
            nc.vector.scalar_tensor_tensor(out=o, in0=i0, scalar=s, in1=i1, op0=op0, op1=op1)

        nc.scalar.dma_start(out=s8[:].rearrange("p (g t) -> p g t", t=4), in_=W_vel_scale.rearrange("o (g p t) -> p (o g) t", p=P, t=4))
        nc.scalar.dma_start(out=b8[:], in_=b_vel.rearrange("(p c) -> p c", c=8))
        for j in range(5):
            load_w(j)
        load_x(0)
        load_x(1)
        for j in range(5, WT):
            load_w(j)
            if j < 7:
                load_x(j - 3)
        nc.sync.dma_start(out=bb[:], in_=b_vel.partition_broadcast(P))

        nc.vector.memset(one[:], 1.0)
        make_identity(nc, ident[:])
        nc.vector.memset(ones[:], 1.0)
        nc.vector.memset(half[:], 0.5)
        nc.scalar.activation(out=warm[:], in_=one[:], func=ACT.Ln)

        nc.scalar.copy(out=wb[1][:, 512:K], in_=wby[1][:, 512:K].bitcast(FP8))
        jb = small("jb", 8)
        nc.scalar.activation(out=jb[:], in_=b8[:], func=ACT.Square, accum_out=pb[:])

        for j, c0 in ((0, 0), (1, 0), (0, 512), (3, 512)):
            cast(nc.vector, j, c0, c0 + 512)
        for j, c0 in ((2, 0), (3, 0), (2, 512)):
            nc.scalar.copy(out=wb[j][:, c0 : c0 + 512], in_=wby[j][:, c0 : c0 + 512].bitcast(FP8))
        for j in range(4, WT):
            cast(nc.gpsimd, j, 0, K)
        def keep_warm(i, count):
            t = bank(i, [P, 512], "warm%d_%d" % (i, count))
            for k in range(count):
                nc.tensor.matmul(out=t[:], lhsT=xin[0][:, 0:P], rhs=xin[0][:, 0:512], start=True, stop=True)

        w_turn(0, 0, (0,))
        w_turn(0, 0, (1,))
        w_turn(0, 1)
        bsq = bank(3, [P, 1], "bsq")
        nc.tensor.matmul(out=bsq[:], lhsT=ones[:], rhs=pb[:], start=True, stop=True)
        w_turn(1, 0)
        x_turn(0)
        x_turn(1)
        w_exit(0, 0, (0,))
        w_turn(1, 1)
        x_turn(2)
        xnorm(0)
        nc.scalar.copy(out=sx[:, RT : RT + 1], in_=bsq[:])
        x_copy(0)
        x_copy(1)
        w_exit(0, 0, (1,))
        w_turn(2, 0)
        x_turn(3)
        x_copy(2)
        xnorm(1)
        x_copy(3)
        for i in range(2, RT):
            xnorm(i)
        w_exit(0, 1)
        w_turn(2, 1)
        keep_warm(0, 2)
        w_exit(1, 0)
        w_turn(3, 0)
        w_exit(1, 1)
        w_turn(3, 1)
        keep_warm(1, 2)
        w_exit(2, 0)
        quant_x()
        quant_w(0)
        for r in range(RT):
            mult(0, r)
        for r in range(RT):
            square(0, r)
        quant_w(1)
        for r in range(RT):
            mult(1, r)
        keep_warm(5, 1)
        n5 = small("n5", 5)
        nc.gpsimd.tensor_scalar(out=n5[:], in0=sx[:], scalar1=EPS, scalar2=None, op0=ALU.max)
        rt = small("rt", 5)
        nc.gpsimd.tensor_tensor(out=rt[:], in0=n5[:], in1=half[:], op=ALU.pow)
        cx = small("cx")
        nc.gpsimd.tensor_scalar(out=cx[:], in0=rt[:, 0:4], scalar1=CMAX, scalar2=None, op0=ALU.min)
        w_exit(2, 1)
        for r in range(RT):
            square(1, r)
        w_exit(3, 0)
        quant_w(2)
        ir = small("ir", 5)
        nc.vector.reciprocal(out=ir[:], in_=rt[:])
        w_exit(3, 1)
        for r in range(RT):
            mult(2, r)
        quant_w(3)

        lnp = small("lnp")
        nc.scalar.activation(out=lnp[:], in_=cx[:], func=ACT.Ln, bias=1.0)
        lnq = small("lnq")
        nc.scalar.activation(out=lnq[:], in_=cx[:], func=ACT.Ln, scale=-1.0, bias=1.0)
        at2 = small("at2")
        nc.gpsimd.tensor_tensor(out=at2[:], in0=lnp[:], in1=lnq[:], op=ALU.subtract)
        kp = small("kp")
        nc.gpsimd.tensor_tensor(out=kp[:], in0=at2[:], in1=ir[:, 0:4], op=ALU.mult)
        tb = small("tb", 1)
        nc.scalar.activation(out=tb[:], in_=rt[:, 4:5], func=ACT.Tanh)
        kap = small("kap")
        nc.scalar.activation(out=kap[:], in_=kp[:], func=ACT.Copy, scale=0.5)
        for r in range(RT):
            square(2, r)
        for r in range(RT):
            mult(3, r)
        s0 = small("s0")
        nc.gpsimd.tensor_scalar(out=s0[:], in0=smp[:, 0, :], scalar1=EPS, scalar2=None, op0=ALU.max)
        s1 = small("s1")
        nc.gpsimd.tensor_tensor(out=s1[:], in0=s0[:], in1=smp[:, 1, :], op=ALU.add)
        s2 = small("s2")
        nc.gpsimd.tensor_tensor(out=s2[:], in0=s1[:], in1=smp[:, 2, :], op=ALU.add)

        ss = small("ss")
        for r in range(RT):
            square(3, r)
            if r % 2 == 1:
                for i in (r - 1, r):
                    nc.scalar.activation(out=ss[:, i : i + 1], in_=smp[:, 3, i : i + 1], func=ACT.Identity, bias=s2[:, i : i + 1])
        bk = small("bk", 2)
        nc.scalar.activation(out=bk[:, 0:1], in_=tb[:], func=ACT.Copy, scale=ir[:, 4:5])
        q2 = small("q2", 1)
        nc.scalar.activation(out=q2[:], in_=tb[:], func=ACT.Square)
        nc.scalar.activation(out=bk[:, 1:2], in_=q2[:], func=ACT.Copy, scale=KF, bias=-KF)
        nbk = small("nbk", 2)
        nc.scalar.activation(out=nbk[:], in_=bk[:], func=ACT.Copy, scale=-1.0)
        q2p1 = small("q2p1", 1)
        nc.scalar.activation(out=q2p1[:], in_=q2[:], func=ACT.Copy, bias=1.0)
        beta = bk[:, 0:1]
        st = []
        for h in range(2):
            d = {}
            for name, w in (("m", 2), ("db", 2), ("rm", 2), ("th", 2), ("t2", 2), ("c1", 2), ("al", 2), ("y", 2), ("u", 6), ("omq", 2), ("den", 2), ("rr", 2), ("v3", 6), ("ff", 4)):
                d[name] = small("%s_%d" % (name, h), w)
            st.append(d)

        def by_rows(t):
            return t[:].rearrange("p (a r) -> p a r", r=2)

        def c_m(h):
            d = st[h]
            nc.gpsimd.tensor_tensor(out=d["m"][:], in0=ss[:, 2 * h : 2 * h + 2], in1=half[:, 0:2], op=ALU.pow)
            for k in range(2):
                nc.scalar.activation(out=d["th"][:, k : k + 1], in_=d["m"][:, k : k + 1], func=ACT.Tanh, scale=kap[:, 2 * h + k : 2 * h + k + 1])
            nc.scalar.activation(out=d["t2"][:], in_=d["th"][:], func=ACT.Square)
            nc.scalar.activation(out=d["c1"][:], in_=d["t2"][:], func=ACT.Identity, scale=q2[:], bias=1.0)
            for i, t in enumerate((d["u"][:, 2:4], d["omq"][:])):
                nc.scalar.activation(out=t, in_=d["t2"][:], func=ACT.Identity, scale=bk[:, i : i + 1], bias=nbk[:, i : i + 1])

        def c_d(h):
            if h == 0:
                vtt(st[h]["db"][:], dp[:, 0, 0:2], dp[:, 1, 0:2], ALU.add)
                return
            for k in range(2):
                r = 2 * h + k
                nc.scalar.activation(out=st[h]["db"][:, k : k + 1], in_=dp[:, 1, r : r + 1], func=ACT.Identity, bias=dp[:, 0, r : r + 1])

        def c_r(h):
            nc.vector.reciprocal(out=st[h]["rm"][:], in_=st[h]["m"][:])

        def c_a(h):
            d = st[h]
            vtt(d["al"][:], d["th"][:], d["rm"][:], ALU.mult)

        def c_y(h):
            d = st[h]
            vstt(d["y"][:], d["al"][:], beta, d["db"][:], ALU.mult, ALU.mult)

        def c_den(h):
            d = st[h]
            vtt(d["den"][:], d["y"][:], d["c1"][:], ALU.add)
            vstt(d["u"][:, 4:6], d["y"][:], q2p1[:], d["al"][:], ALU.add, ALU.mult)

        def c_g(h):
            d = st[h]
            nc.vector.reciprocal(out=d["rr"][:], in_=d["den"][:])
            vstt(d["u"][:, 0:2], d["den"][:], 1.5 - KF, d["omq"][:], ALU.mult, ALU.add)

        def c_v(h):
            d = st[h]
            vstt(by_rows(d["v3"]), d["rr"][:].unsqueeze(1).to_broadcast([P, 3, 2]), BIG, by_rows(d["u"]), ALU.min, ALU.mult)

        def c_f(h):
            d = st[h]
            vstt(by_rows(d["ff"]), by_rows(d["v3"])[:, 0:1, :].to_broadcast([P, 2, 2]), 1.0, by_rows(d["v3"])[:, 1:3, :], ALU.min, ALU.mult)

        bqs = {}

        def prod_b(c, r, on_vector=False):
            nfb = st[r // 2]["ff"][:, r % 2 : r % 2 + 1]
            bq = outp.tile([P, 512], F32, name="bq")
            if on_vector:
                vts(bq[:], bb[:, 512 * c : 512 * (c + 1)], nfb, None, ALU.mult)
            else:
                nc.scalar.activation(out=bq[:], in_=bb[:, 512 * c : 512 * (c + 1)], func=ACT.Copy, scale=nfb)
            bqs[(c, r)] = bq

        def final(c, r):
            fa = st[r // 2]["ff"][:, 2 + r % 2 : 3 + r % 2]
            o = outp.tile([P, 512], F32, name="o")
            vstt(o[:], mx[(c, r)][:], fa, bqs[(c, r)][:], ALU.mult, ALU.subtract)
            nc.sync.dma_start(out=out[P * r : P * (r + 1), 512 * c : 512 * (c + 1)], in_=o[:])

        c_m(0)
        dot(0, 0)
        dot(0, 1)
        dot(0, 2)
        dot(1, 0)
        dot(1, 1)
        c_r(0)
        c_d(0)
        c_m(1)
        dot(0, 3)
        c_a(0)
        dot(1, 2)
        c_y(0)
        c_r(1)
        dot(1, 3)
        c_den(0)
        c_d(1)
        c_a(1)
        c_g(0)
        c_v(0)
        c_y(1)
        c_f(0)
        c_den(1)
        prod_b(0, 0, on_vector=True)
        for c, r in ((1, 0), (0, 1), (1, 1)):
            prod_b(c, r)
        c_g(1)
        final(0, 0)
        c_v(1)
        final(1, 0)
        c_f(1)
        final(0, 1)
        final(1, 1)
        for r in (2, 3):
            for c in range(2):
                prod_b(c, r)
                final(c, r)
